import numpy as np
import ml_dtypes


def mxq(x, axis, fmt="e4m3"):
    dtype, down = {"e4m3": (ml_dtypes.float8_e4m3fn, 7), "e5m2": (ml_dtypes.float8_e5m2, 14)}[fmt]
    v = np.moveaxis(np.asarray(x, np.float32).astype(ml_dtypes.bfloat16).astype(np.float64), axis, -1)
    blocks = v.reshape(v.shape[:-1] + (-1, 32))
    amax = np.abs(blocks).max(-1, keepdims=True)
    byte = np.maximum(np.where(amax > 0, np.frexp(amax)[1] - 1 + 127, 0) - down, 1)
    scale = np.exp2(byte - 127.0)
    codes = (blocks / scale).astype(np.float32).astype(dtype).astype(np.float64)
    return np.moveaxis((codes * scale).reshape(v.shape), -1, axis)


WIDE = False


def mx_kscale(k):
    if not WIDE:
        return np.ones(k)
    levels = np.array([10, -10, 5, -5, 0])
    a = np.random.permutation(np.resize(levels, k // 512 * 4)).reshape(k // 512, 4)
    idx = np.arange(k)
    return np.exp2(a[idx // 512, idx % 128 // 32])


BF16 = ml_dtypes.bfloat16


def bf(x):
    return np.asarray(x, np.float32).astype(BF16)


def f64(x):
    return np.asarray(x).astype(np.float64)


B, S, D, H, DN, DR, DV, QL, KVL, LBLK = 4, 256, 2048, 16, 128, 64, 128, 512, 512, 64
DKV = DN + DV


def silu(v):
    return v / (1.0 + np.exp(-v))


def eta(t):
    m = t.reshape(t.shape[0], H, -1).max(-1)
    m = np.where(m == 0, 1e-6, m)
    return np.minimum(10.0 / m, 1.0)


def setup_inputs():
    s, t = mx_kscale(D), mx_kscale(KVL)
    amp = np.linspace(0.5, 1.5, S)[None, :, None]
    return {"x": bf(np.random.standard_normal((B, S, D)) * amp * s),
            "wkv_c": bf(np.random.standard_normal((KVL, D)) / np.sqrt(D) / s[None, :] * t[:, None]),
            "wkv_b": bf(np.random.standard_normal((H * DKV, KVL)) * 2.5 / np.sqrt(KVL) / t[None, :])}


def reference(x, wkv_c, wkv_b):
    kv_c = mxq(f64(x), 2, "e4m3") @ mxq(f64(wkv_c), 1, "e4m3").T
    kv = (mxq(kv_c, 2, "e4m3") @ mxq(f64(wkv_b), 1, "e4m3").T).reshape(B, S, H, DKV)
    k, v = silu(kv[..., :DN]), kv[..., DN:]
    return k * eta(k)[:, None, :, None], v

@@ -1,0 +1,670 @@
+from contextlib import ExitStack
+
+import concourse.mybir as mybir
+from concourse.masks import make_identity
+
+F32 = mybir.dt.float32
+BF16 = mybir.dt.bfloat16
+U32 = mybir.dt.uint32
+U8 = mybir.dt.uint8
+FP8X4 = mybir.dt.float8_e4m3fn_x4
+ACT = mybir.ActivationFunctionType
+ALU = mybir.AluOpType
+AX = mybir.AxisListType
+
+P = 128
+B, S, D, H, KVL = 4, 256, 2048, 16, 512
+G = D // 512
+FLOPS = 2 * B * S * D * KVL + 2 * B * S * KVL * H * 256
+NSLAB = 18
+MUL = ["GG","GG","GG","VGVS"]
+
+ORDER = [
+    ("Lx0a", "q", -1, -1),
+    ("Lx0b", "q", -1, -1),
+    ("Lwc00", "q", -1, -1),
+    ("Lwc01", "q", -1, -1),
+    ("Lwc10", "q", -1, -1),
+    ("Lwc11", "q", -1, -1),
+    ("Lwb00", "q", -1, -1),
+    ("Lwb01", "q", -1, -1),
+    ("Lwb10", "q", -1, -1),
+    ("Tx00", "p", 0, 0),
+    ("Lwb11", "q", -1, -1),
+    ("Tx01", "p", 1, -1),
+    ("ex00", "s", -1, -1),
+    ("ex01", "v", -1, -1),
+    ("Tx02", "p", 2, 1),
+    ("Lx1", "q", -1, -1),
+    ("Tx03", "p", 3, -1),
+    ("qx00", "v", -1, -1),
+    ("ex02", "s", -1, -1),
+    ("ex03", "v", -1, -1),
+    ("Twc00", "p", 4, 2),
+    ("Lx2", "q", -1, -1),
+    ("Twc10", "p", 5, 3),
+    ("qx01", "v", -1, -1),
+    ("ewc00", "s", -1, -1),
+    ("ewc10", "v", -1, -1),
+    ("Twc01", "p", 6, -1),
+    ("Lx3", "q", -1, -1),
+    ("Twc11", "p", 7, -1),
+    ("ewc01", "s", -1, -1),
+    ("ewc11", "v", -1, -1),
+    ("Twc20", "p", 0, 4),
+    ("Twc30", "p", 1, 0),
+    ("qwc0", "v", -1, -1),
+    ("ewc20", "s", -1, -1),
+    ("qwc1", "v", -1, -1),
+    ("Twc21", "p", 2, -1),
+    ("ewc30", "s", -1, -1),
+    ("Twc31", "p", 3, -1),
+    ("ewc21", "s", -1, -1),
+    ("ewc31", "v", -1, -1),
+    ("qwc2", "v", -1, -1),
+    ("qwc3", "v", -1, -1),
+    ("Twb000", "p", 4, 1),
+    ("Twb001", "p", 5, -1),
+    ("ewb000", "s", -1, -1),
+    ("M100", "p", 6, -1),
+    ("ewb001", "v", -1, -1),
+    ("qwb00", "v", -1, -1),
+    ("M101", "p", 7, -1),
+    ("kve00", "s", -1, -1),
+    ("qkv00", "v", -1, -1),
+    ("Twb010", "p", 0, 2),
+    ("kve01", "s", -1, -1),
+    ("Twb011", "p", 1, -1),
+    ("ewb010", "v", -1, -1),
+    ("Twb020", "p", 2, 3),
+    ("ewb011", "s", -1, -1),
+    ("Twb021", "p", 3, -1),
+    ("qkv01", "v", -1, -1),
+    ("Twb030", "p", 4, 4),
+    ("ewb020", "v", -1, -1),
+    ("ewb021", "s", -1, -1),
+    ("Twb031", "p", 5, -1),
+    ("qwb01", "v", -1, -1),
+    ("M20000", "p", 6, -1),
+    ("ewb030", "s", -1, -1),
+    ("M20100", "p", 7, -1),
+    ("qwb02", "v", -1, -1),
+    ("M20001", "p", 0, -1),
+    ("ewb031", "s", -1, -1),
+    ("M20101", "p", 1, -1),
+    ("Twb100", "p", 2, 0),
+    ("o0000", "s", -1, -1),
+    ("qwb03", "v", -1, -1),
+    ("M20002", "p", 3, -1),
+    ("o0100", "s", -1, -1),
+    ("ewb100", "v", -1, -1),
+    ("M20102", "p", 4, -1),
+    ("M20003", "p", 5, -1),
+    ("o0001", "s", -1, -1),
+    ("M20103", "p", 6, -1),
+    ("Twb101", "p", 7, -1),
+    ("o0101", "s", -1, -1),
+    ("mx000", "v", -1, -1),
+    ("Twb110", "p", 2, 1),
+    ("o0002", "s", -1, -1),
+    ("Tx10", "p", 0, 2),
+    ("Tx11", "p", 1, -1),
+    ("o0102", "s", -1, -1),
+    ("mx010", "v", -1, -1),
+    ("Tx12", "p", 3, 3),
+    ("o0003", "s", -1, -1),
+    ("Tx13", "p", 4, -1),
+    ("o0103", "s", -1, -1),
+    ("ex10", "v", -1, -1),
+    ("Twb111", "p", 5, -1),
+    ("ex11", "s", -1, -1),
+    ("mx001", "v", -1, -1),
+    ("Twb120", "p", 6, 4),
+    ("Twb121", "p", 0, -1),
+    ("ex12", "s", -1, -1),
+    ("ex13", "s", -1, -1),
+    ("mx011", "v", -1, -1),
+    ("ewb101", "s", -1, -1),
+    ("ewb110", "s", -1, -1),
+    ("E10", "v", -1, -1),
+    ("qx10", "v", -1, -1),
+    ("ET0", "p", 1, -1),
+    ("ewb111", "s", -1, -1),
+    ("E20", "v", -1, -1),
+    ("Twb130", "p", 3, 2),
+    ("ewb120", "s", -1, -1),
+    ("Twb131", "p", 4, -1),
+    ("qx11", "v", -1, -1),
+    ("mu000", "g", -1, -1),
+    ("ewb121", "s", -1, -1),
+    ("qwb10", "v", -1, -1),
+    ("M110", "p", 7, -1),
+    ("ewb130", "s", -1, -1),
+    ("qwb11", "v", -1, -1),
+    ("ewb131", "s", -1, -1),
+    ("qwb12", "v", -1, -1),
+    ("M111", "p", 2, -1),
+    ("mu001", "g", -1, -1),
+    ("kve10", "s", -1, -1),
+    ("qwb13", "v", -1, -1),
+    ("Sk000", "q", -1, -1),
+    ("qkv10", "v", -1, -1),
+    ("M20010", "p", 5, -1),
+    ("M20110", "p", 1, -1),
+    ("kve11", "s", -1, -1),
+    ("M20011", "p", 6, -1),
+    ("o0010", "v", -1, -1),
+    ("M20111", "p", 0, -1),
+    ("o0110", "s", -1, -1),
+    ("M20012", "p", 3, -1),
+    ("qkv11", "v", -1, -1),
+    ("mu010", "g", -1, -1),
+    ("Sk001", "q", -1, -1),
+    ("o0011", "v", -1, -1),
+    ("M20112", "p", 4, -1),
+    ("o0111", "s", -1, -1),
+    ("M20013", "p", 7, -1),
+    ("o0012", "v", -1, -1),
+    ("M20113", "p", 2, -1),
+    ("Sv000", "q", -1, -1),
+    ("o0112", "s", -1, -1),
+    ("Sv010", "q", -1, -1),
+    ("M21000", "p", 5, -1),
+    ("o0013", "v", -1, -1),
+    ("M21001", "p", 1, -1),
+    ("o0113", "s", -1, -1),
+    ("M21002", "p", 6, -1),
+    ("M21003", "p", 0, -1),
+    ("Sv001", "q", -1, -1),
+    ("o1000", "s", -1, -1),
+    ("Sv011", "q", -1, -1),
+    ("M21100", "p", 3, -1),
+    ("mu011", "g", -1, -1),
+    ("Sk010", "q", -1, -1),
+    ("M21101", "p", 4, -1),
+    ("o1001", "s", -1, -1),
+    ("M21102", "p", 7, -1),
+    ("M21103", "p", 2, -1),
+    ("o1002", "s", -1, -1),
+    ("mx100", "v", -1, -1),
+    ("Tx20", "p", 5, 3),
+    ("o1003", "s", -1, -1),
+    ("Tx21", "p", 1, -1),
+    ("Tx22", "p", 6, 0),
+    ("o1100", "s", -1, -1),
+    ("ex20", "v", -1, -1),
+    ("Tx23", "p", 0, -1),
+    ("Sk011", "q", -1, -1),
+    ("o1101", "s", -1, -1),
+    ("mx101", "v", -1, -1),
+    ("M21010", "p", 3, -1),
+    ("M21011", "p", 5, -1),
+    ("o1102", "s", -1, -1),
+    ("M21012", "p", 4, -1),
+    ("o1103", "s", -1, -1),
+    ("mx110", "v", -1, -1),
+    ("M21013", "p", 7, -1),
+    ("ex21", "s", -1, -1),
+    ("M21110", "p", 2, -1),
+    ("ex22", "s", -1, -1),
+    ("mx111", "v", -1, -1),
+    ("M21111", "p", 1, -1),
+    ("ex23", "s", -1, -1),
+    ("M21112", "p", 6, -1),
+    ("o1010", "s", -1, -1),
+    ("E11", "v", -1, -1),
+    ("M21113", "p", 0, -1),
+    ("qx20", "v", -1, -1),
+    ("o1011", "s", -1, -1),
+    ("ET1", "p", 3, -1),
+    ("qx21", "v", -1, -1),
+    ("o1012", "s", -1, -1),
+    ("Tx30", "p", 5, 1),
+    ("Sv100", "q", -1, -1),
+    ("E21", "v", -1, -1),
+    ("o1013", "s", -1, -1),
+    ("M120", "p", 4, -1),
+    ("o1110", "v", -1, -1),
+    ("mu100", "g", -1, -1),
+    ("o1111", "s", -1, -1),
+    ("Sv101", "q", -1, -1),
+    ("o1112", "v", -1, -1),
+    ("o1113", "s", -1, -1),
+    ("Sv110", "q", -1, -1),
+    ("M121", "p", 3, -1),
+    ("ex30", "v", -1, -1),
+    ("kve20", "s", -1, -1),
+    ("Sv111", "q", -1, -1),
+    ("qkv20", "v", -1, -1),
+    ("mu101", "g", -1, -1),
+    ("Tx31", "p", 7, -1),
+    ("Sk100", "q", -1, -1),
+    ("kve21", "s", -1, -1),
+    ("M22000", "p", 2, -1),
+    ("ex31", "v", -1, -1),
+    ("M22001", "p", 1, -1),
+    ("M22002", "p", 6, -1),
+    ("o2000", "s", -1, -1),
+    ("qkv21", "v", -1, -1),
+    ("M22003", "p", 0, -1),
+    ("qx30", "v", -1, -1),
+    ("M22100", "p", 5, -1),
+    ("o2001", "s", -1, -1),
+    ("M22101", "p", 4, -1),
+    ("mu110", "g", -1, -1),
+    ("M22102", "p", 3, -1),
+    ("Sk101", "q", -1, -1),
+    ("o2002", "s", -1, -1),
+    ("mx200", "v", -1, -1),
+    ("M22103", "p", 7, -1),
+    ("Tx32", "p", 2, 4),
+    ("o2003", "s", -1, -1),
+    ("Tx33", "p", 1, -1),
+    ("o2100", "s", -1, -1),
+    ("mx201", "v", -1, -1),
+    ("M22010", "p", 6, -1),
+    ("M22011", "p", 0, -1),
+    ("o2101", "s", -1, -1),
+    ("M22012", "p", 5, -1),
+    ("mu111", "g", -1, -1),
+    ("Sk110", "q", -1, -1),
+    ("o2102", "s", -1, -1),
+    ("ex32", "v", -1, -1),
+    ("M22013", "p", 4, -1),
+    ("o2103", "s", -1, -1),
+    ("mx210", "v", -1, -1),
+    ("M22110", "p", 3, -1),
+    ("M22111", "p", 2, -1),
+    ("ex33", "s", -1, -1),
+    ("M22112", "p", 7, -1),
+    ("o2010", "s", -1, -1),
+    ("mx211", "v", -1, -1),
+    ("M22113", "p", 1, -1),
+    ("Sk111", "q", -1, -1),
+    ("o2011", "s", -1, -1),
+    ("o2012", "s", -1, -1),
+    ("E12", "v", -1, -1),
+    ("Sv200", "q", -1, -1),
+    ("qx31", "v", -1, -1),
+    ("ET2", "p", 6, -1),
+    ("o2013", "s", -1, -1),
+    ("o2110", "v", -1, -1),
+    ("M130", "p", 0, -1),
+    ("o2111", "s", -1, -1),
+    ("Sv201", "q", -1, -1),
+    ("E22", "v", -1, -1),
+    ("o2112", "s", -1, -1),
+    ("Sv210", "q", -1, -1),
+    ("o2113", "v", -1, -1),
+    ("mu200", "g", -1, -1),
+    ("M131", "p", 5, -1),
+    ("kve30", "s", -1, -1),
+    ("Sv211", "q", -1, -1),
+    ("qkv30", "v", -1, -1),
+    ("M23000", "p", 4, -1),
+    ("M23001", "p", 3, -1),
+    ("kve31", "s", -1, -1),
+    ("M23002", "p", 2, -1),
+    ("mu201", "g", -1, -1),
+    ("M23003", "p", 6, -1),
+    ("Sk200", "q", -1, -1),
+    ("o3000", "s", -1, -1),
+    ("qkv31", "v", -1, -1),
+    ("M23010", "p", 7, -1),
+    ("M23100", "p", 1, -1),
+    ("o3001", "s", -1, -1),
+    ("M23101", "p", 0, -1),
+    ("o3010", "v", -1, -1),
+    ("M23102", "p", 5, -1),
+    ("o3002", "s", -1, -1),
+    ("M23103", "p", 4, -1),
+    ("mx300", "v", -1, -1),
+    ("M23011", "p", 3, -1),
+    ("o3003", "s", -1, -1),
+    ("M23012", "p", 7, -1),
+    ("mu210", "g", -1, -1),
+    ("Sk201", "q", -1, -1),
+    ("M23013", "p", 2, -1),
+    ("o3100", "s", -1, -1),
+    ("M23110", "p", 6, -1),
+    ("mx301", "v", -1, -1),
+    ("o3101", "s", -1, -1),
+    ("M23111", "p", 1, -1),
+    ("o3102", "s", -1, -1),
+    ("M23112", "p", 0, -1),
+    ("mx310", "v", -1, -1),
+    ("o3103", "s", -1, -1),
+    ("M23113", "p", 5, -1),
+    ("mu211", "g", -1, -1),
+    ("Sk210", "q", -1, -1),
+    ("o3011", "s", -1, -1),
+    ("mx311", "v", -1, -1),
+    ("o3012", "s", -1, -1),
+    ("Sv300", "q", -1, -1),
+    ("o3013", "s", -1, -1),
+    ("E13", "v", -1, -1),
+    ("o3110", "v", -1, -1),
+    ("ET3", "p", 4, -1),
+    ("o3111", "s", -1, -1),
+    ("Sv301", "q", -1, -1),
+    ("Sk211", "q", -1, -1),
+    ("o3112", "v", -1, -1),
+    ("o3113", "s", -1, -1),
+    ("Sv310", "q", -1, -1),
+    ("E23", "v", -1, -1),
+    ("Sv311", "q", -1, -1),
+    ("mu300", "v", -1, -1),
+    ("mu303", "s", -1, -1),
+    ("mu301", "g", -1, -1),
+    ("mu302", "v", -1, -1),
+    ("Sk300", "q", -1, -1),
+    ("mu313", "s", -1, -1),
+    ("mu310", "v", -1, -1),
+    ("mu311", "g", -1, -1),
+    ("Sk303", "q", -1, -1),
+    ("Sk301", "q", -1, -1),
+    ("Sk302", "q", -1, -1),
+    ("mu312", "v", -1, -1),
+    ("Sk310", "q", -1, -1),
+    ("Sk311", "q", -1, -1),
+    ("Sk312", "q", -1, -1),
+    ("Sk313", "q", -1, -1),
+]
+
+
+def tile_ssa_pb_kernel(tc, x, wkv_c, wkv_b, out_0, out_1):
+    nc = tc.nc
+    with ExitStack() as ctx:
+        const = ctx.enter_context(tc.tile_pool(name="const", bufs=1))
+        slabs = ctx.enter_context(tc.tile_pool(name="slabs", bufs=NSLAB))
+        stage = ctx.enter_context(tc.tile_pool(name="stage", bufs=1))
+        keep = ctx.enter_context(tc.tile_pool(name="keep", bufs=1))
+        small = ctx.enter_context(tc.tile_pool(name="small", bufs=2))
+        psum = ctx.enter_context(tc.psum_pool(name="psum", bufs=1))
+        ctx.enter_context(tc.manual_schedule())
+
+        x_view = x.rearrange("b (p r) d -> b p r d", r=2)
+        wc_view = wkv_c.rearrange("(u p e) d -> u p e d", u=2, e=2)
+        wb_view = wkv_b.rearrange("(h v c) k -> v c h k", v=2, c=P)
+        k_view = out_0.rearrange("b (p r) h d -> b r p (h d)", r=2)
+        v_view = out_1.rearrange("b (p r) h d -> b r p (h d)", r=2)
+
+        ident = const.tile([P, P], F32, name="ident")
+        make_identity(nc, ident[:])
+        warm = const.tile([P, 2], F32, name="warm")
+        nc.vector.memset(warm[:], 0.0)
+        nc.scalar.activation(out=warm[:, 1:2], in_=warm[:, 0:1], func=ACT.Silu)
+
+        wc_codes = keep.tile([P, G, KVL], U32, name="wc_codes", align_bytes=64)
+        wc_scales = keep.tile([P, G, KVL], U8, name="wc_scales", align_bytes=64)
+        x_codes = keep.tile([P, B, G, S], U32, name="x_codes", align_bytes=64)
+        x_scales = keep.tile([P, B, G, S], U8, name="x_scales", align_bytes=64)
+        wb_codes = keep.tile([P, 2, H * P], U32, name="wb_codes", align_bytes=64)
+        wb_scales = keep.tile([P, 2, H * P], U8, name="wb_scales", align_bytes=64)
+        kv_codes = keep.tile([P, B, S], U32, name="kv_codes", align_bytes=64)
+        kv_scales = keep.tile([P, B, S], U8, name="kv_scales", align_bytes=64)
+
+        live = {}
+
+        def slab(key, shape, dtype):
+            if key not in live:
+                live[key] = slabs.tile(shape, dtype, name="slab_" + key, tag="slab")
+            return live[key]
+
+        def bank(key, ps, shape):
+            live[key] = psum.tile(shape, F32, name="bank_" + key, tag="ps%d" % ps)
+            return live[key]
+
+        def evac(engine, out, in_):
+            if engine == "v":
+                nc.vector.tensor_copy(out=out, in_=in_)
+            else:
+                nc.scalar.copy(out=out, in_=in_)
+
+        def load(name):
+            if name[0] == "x":
+                b = int(name[1])
+                t = slab("x%d" % b, [P, 2, D], BF16)
+                if b == 0:
+                    half = 0 if name[2] == "a" else 1
+                    cols = slice(1024 * half, 1024 * half + 1024)
+                    nc.sync.dma_start(out=t[:, :, cols], in_=x_view[b, :, :, cols])
+                else:
+                    nc.sync.dma_start(out=t[:], in_=x_view[b])
+            elif name[:2] == "wc":
+                half, u = int(name[2]), int(name[3])
+                t = slab("wc%d" % half, [P, 2, 2, 1024], BF16)
+                nc.sync.dma_start(
+                    out=t[:, u], in_=wc_view[u, :, :, 1024 * half : 1024 * half + 1024]
+                )
+            else:
+                v, half = int(name[2]), int(name[3])
+                t = slab(name, [P, 8, KVL], BF16)
+                nc.sync.dma_start(out=t[:], in_=wb_view[v, :, 8 * half : 8 * half + 8, :])
+
+        def words(ap, first):
+            return ap.bitcast(F32)[:, first : first + P]
+
+        def group_of(name):
+            if name[0] == "x":
+                g = int(name[2])
+                return "x%s%d" % (name[1], g // 2), g % 2
+            if name[:2] == "wc":
+                return name[:3], int(name[3])
+            return name[:4], int(name[4])
+
+        def sources(name):
+            if name[0] == "x":
+                b, g = int(name[1]), int(name[2])
+                return [
+                    words(live["x%d" % b][:, r, :], 256 * g + P * u)
+                    for r in range(2)
+                    for u in range(2)
+                ]
+            if name[:2] == "wc":
+                g, u = int(name[2]), int(name[3])
+                return [
+                    words(live["wc%d" % (g // 2)][:, u, e, :], 256 * (g % 2) + P * u2)
+                    for e in range(2)
+                    for u2 in range(2)
+                ]
+            v, hq, pp = int(name[2]), int(name[3]), int(name[4])
+            srcs = []
+            for hh in range(2):
+                h = 4 * hq + 2 * pp + hh
+                for u in range(2):
+                    srcs.append(words(live["wb%d%d" % (v, h // 8)][:, h % 8, :], P * u))
+            return srcs
+
+        def flip(name, ps, grp):
+            key, half = group_of(name)
+            if half == 0:
+                live["g" + key] = stage.tile(
+                    [P, 2048], BF16, name="grp_" + key, tag="grp%d" % grp, align_bytes=64
+                )
+            t = bank("T" + name, ps, [P, 4, P])
+            srcs = sources(name)
+            for i in range(4):
+                nc.tensor.transpose(t[:, i, :], srcs[i], ident[:])
+
+        def flip_out(name, engine):
+            key, half = group_of(name)
+            dst = live["g" + key][:].bitcast(F32).rearrange("q (a c u) -> q a c u", a=4, u=2)
+            evac(
+                engine,
+                dst[:, 2 * half : 2 * half + 2],
+                live["T" + name][:].rearrange("q (a u) c -> q a c u", u=2),
+            )
+
+        def quantise(key):
+            if key[0] == "x":
+                b, gp = int(key[1]), int(key[2])
+                codes = x_codes[:, b, 2 * gp : 2 * gp + 2, :].rearrange("q g s -> q (g s)")
+                scales = x_scales[:, b, 2 * gp : 2 * gp + 2, :].rearrange("q g s -> q (g s)")
+            elif key[:2] == "wc":
+                g = int(key[2])
+                codes, scales = wc_codes[:, g, :], wc_scales[:, g, :]
+            else:
+                v, hq = int(key[2]), int(key[3])
+                cols = slice(512 * hq, 512 * hq + 512)
+                codes, scales = wb_codes[:, v, cols], wb_scales[:, v, cols]
+            nc.vector.quantize_mx(out=codes.bitcast(FP8X4), scales=scales, in_=live["g" + key][:])
+
+        def stage1(b, r, ps):
+            acc = bank("M1%d%d" % (b, r), ps, [P, 4, P])
+            toks = slice(P * r, P * r + P)
+            for j in range(4):
+                rows = slice(P * j, P * j + P)
+                for g in range(G):
+                    nc.tensor.matmul_mx(
+                        out=acc[:, j, :],
+                        lhsT=wc_codes[:, g, rows].bitcast(FP8X4),
+                        lhsT_scale=wc_scales[:, g, rows],
+                        rhs=x_codes[:, b, g, toks].bitcast(FP8X4),
+                        rhs_scale=x_scales[:, b, g, toks],
+                        start=(g == 0),
+                        stop=(g == G - 1),
+                    )
+
+        def stage1_out(b, r, engine):
+            kvg = stage.tile([P, P, 4], BF16, name="kvg%d%d" % (b, r), tag="kvg", bufs=3, align_bytes=64)
+            live["kvg%d%d" % (b, r)] = kvg
+            evac(engine, kvg[:], live["M1%d%d" % (b, r)][:].rearrange("q j t -> q t j"))
+
+        def stage1_quantise(b, r):
+            toks = slice(P * r, P * r + P)
+            nc.vector.quantize_mx(
+                out=kv_codes[:, b, toks].bitcast(FP8X4),
+                scales=kv_scales[:, b, toks],
+                in_=live["kvg%d%d" % (b, r)][:].rearrange("q t j -> q (t j)"),
+            )
+
+        def product(b, r, v, hq, ps):
+            t = bank("M2%d%d%d%d" % (b, r, v, hq), ps, [P, 512])
+            toks = slice(P * r, P * r + P)
+            cols = slice(512 * hq, 512 * hq + 512)
+            nc.tensor.matmul_mx(
+                out=t[:],
+                lhsT=kv_codes[:, b, toks].bitcast(FP8X4),
+                lhsT_scale=kv_scales[:, b, toks],
+                rhs=wb_codes[:, v, cols].bitcast(FP8X4),
+                rhs_scale=wb_scales[:, v, cols],
+                start=True,
+                stop=True,
+            )
+
+        def product_out(b, r, v, hq, engine):
+            t = live["M2%d%d%d%d" % (b, r, v, hq)]
+            dst = slab("%s%d%d" % ("av"[v], b, r), [P, H * P], F32)
+            cols = slice(512 * hq, 512 * hq + 512)
+            if v == 0:
+                nc.scalar.activation(out=dst[:, cols], in_=t[:], func=ACT.Silu)
+            else:
+                evac(engine, dst[:, cols], t[:])
+
+        def part_max(b, r, h):
+            if "pm%d" % b not in live:
+                live["pm%d" % b] = small.tile([P, 4], F32, name="pm%d" % b, tag="pm")
+            i = 2 * r + h
+            nc.vector.tensor_reduce(
+                out=live["pm%d" % b][:, i : i + 1],
+                in_=live["a%d%d" % (b, r)][:, 1024 * h : 1024 * h + 1024],
+                axis=AX.X,
+                op=ALU.max,
+            )
+
+        def spread_max(b):
+            tokmax = small.tile([P, 1], F32, name="tokmax%d" % b, tag="tokmax")
+            nc.vector.tensor_reduce(out=tokmax[:], in_=live["pm%d" % b][:], axis=AX.X, op=ALU.max)
+            spread = small.tile([P, P], F32, name="spread%d" % b, tag="spread")
+            nc.vector.tensor_copy(out=spread[:], in_=tokmax[:].to_broadcast([P, P]))
+            live["spread%d" % b] = spread
+
+        def flip_max(b, ps):
+            t = bank("ET%d" % b, ps, [P, 4, P])
+            nc.tensor.transpose(t[:, 0, :], live["spread%d" % b][:], ident[:])
+
+        def factors(b):
+            m = small.tile([P, H], F32, name="m%d" % b, tag="m")
+            nc.vector.tensor_reduce(
+                out=m[:],
+                in_=live["ET%d" % b][:, 0, :].rearrange("q (g s) -> q g s", s=8),
+                axis=AX.X,
+                op=ALU.max,
+            )
+            z = small.tile([P, H], F32, name="z%d" % b, tag="z")
+            nc.vector.tensor_scalar(
+                out=z[:], in0=m[:], scalar1=0.0, scalar2=1e-6, op0=ALU.is_equal, op1=ALU.mult
+            )
+            nc.vector.tensor_tensor(out=z[:], in0=z[:], in1=m[:], op=ALU.add)
+            rc = small.tile([P, H], F32, name="rc%d" % b, tag="rc")
+            nc.vector.reciprocal(out=rc[:], in_=z[:])
+            eta = small.tile([P, H], F32, name="eta%d" % b, tag="eta")
+            nc.vector.tensor_scalar(
+                out=eta[:], in0=rc[:], scalar1=10.0, scalar2=1.0, op0=ALU.mult, op1=ALU.min
+            )
+            live["eta%d" % b] = eta
+
+        def scale_heads(b, r, k, engine):
+            n = H // len(MUL[b])
+            h0 = n * k
+            a, eta = live["a%d%d" % (b, r)], live["eta%d" % b]
+            a3 = a[:, P * h0 : P * (h0 + n)].rearrange("p (h d) -> p h d", h=n)
+            e3 = eta[:, h0 : h0 + n].unsqueeze(2).to_broadcast([P, n, P])
+            if engine == "g":
+                nc.gpsimd.tensor_tensor(out=a3, in0=a3, in1=e3, op=ALU.mult)
+            elif engine == "v":
+                nc.vector.tensor_tensor(out=a3, in0=a3, in1=e3, op=ALU.mult)
+            else:
+                for h in range(h0, h0 + n):
+                    nc.scalar.activation(
+                        out=a[:, P * h : P * h + P],
+                        in_=a[:, P * h : P * h + P],
+                        func=ACT.Copy,
+                        scale=eta[:, h : h + 1],
+                    )
+
+        def store_keys(b, r, k):
+            n = H // len(MUL[b])
+            cols = slice(P * n * k, P * n * (k + 1))
+            nc.sync.dma_start(out=k_view[b, r, :, cols], in_=live["a%d%d" % (b, r)][:, cols])
+
+        def store_values(b, r, h):
+            cols = slice(1024 * h, 1024 * h + 1024)
+            nc.sync.dma_start(out=v_view[b, r, :, cols], in_=live["v%d%d" % (b, r)][:, cols])
+
+        for name, engine, ps, grp in ORDER:
+            d = [int(c) for c in name if c in "0123456789"]
+            if name[0] == "L":
+                load(name[1:])
+            elif name[0] == "T":
+                flip(name[1:], ps, grp)
+            elif name[0] == "e":
+                flip_out(name[1:], engine)
+            elif name[:3] == "qkv":
+                stage1_quantise(d[0], d[1])
+            elif name[0] == "q":
+                quantise(name[1:])
+            elif name[:2] == "M1":
+                stage1(d[1], d[2], ps)
+            elif name[:3] == "kve":
+                stage1_out(d[0], d[1], engine)
+            elif name[:2] == "M2":
+                product(d[1], d[2], d[3], d[4], ps)
+            elif name[0] == "o":
+                product_out(d[0], d[1], d[2], d[3], engine)
+            elif name[:2] == "mx":
+                part_max(d[0], d[1], d[2])
+            elif name[:2] == "Sv":
+                store_values(d[0], d[1], d[2])
+            elif name[:2] == "E1":
+                spread_max(d[1])
+            elif name[:2] == "ET":
+                flip_max(d[0], ps)
+            elif name[:2] == "E2":
+                factors(d[1])
+            elif name[:2] == "mu":
+                scale_heads(d[0], d[1], d[2], engine)
+            else:
+                assert name[:2] == "Sk"
+                store_keys(d[0], d[1], d[2])

@@ -17,358 +17,363 @@ B, S, D, H, KVL = 4, 256, 2048, 16, 512
 G = D // 512
 FLOPS = 2 * B * S * D * KVL + 2 * B * S * KVL * H * 256
 NSLAB = 18
-MUL = ["GG","GG","GG","VGVS"]
+MUL = ["GGGG","GGGG","GGGG","VGVS"]
 
 ORDER = [
-    ("Lx0a", "q", -1, -1),
-    ("Lx0b", "q", -1, -1),
-    ("Lwc00", "q", -1, -1),
-    ("Lwc01", "q", -1, -1),
-    ("Lwc10", "q", -1, -1),
-    ("Lwc11", "q", -1, -1),
+    ("Lx0", "q", -1, -1),
+    ("Lwc0", "q", -1, -1),
+    ("Lwc1", "q", -1, -1),
     ("Lwb00", "q", -1, -1),
     ("Lwb01", "q", -1, -1),
     ("Lwb10", "q", -1, -1),
-    ("Tx00", "p", 0, 0),
     ("Lwb11", "q", -1, -1),
-    ("Tx01", "p", 1, -1),
-    ("ex00", "s", -1, -1),
-    ("ex01", "v", -1, -1),
-    ("Tx02", "p", 2, 1),
     ("Lx1", "q", -1, -1),
-    ("Tx03", "p", 3, -1),
-    ("qx00", "v", -1, -1),
-    ("ex02", "s", -1, -1),
-    ("ex03", "v", -1, -1),
-    ("Twc00", "p", 4, 2),
     ("Lx2", "q", -1, -1),
+    ("Lx3", "q", -1, -1),
+    ("Tx00", "p", 0, 0),
+    ("Tx01", "p", 1, -1),
+    ("Tx02", "p", 2, 1),
+    ("ex00", "s", -1, -1),
+    ("Tx03", "p", 3, -1),
+    ("ex01", "v", -1, -1),
+    ("ex02", "s", -1, -1),
+    ("qx00", "v", -1, -1),
+    ("ex03", "s", -1, -1),
+    ("Twc00", "p", 4, 2),
     ("Twc10", "p", 5, 3),
     ("qx01", "v", -1, -1),
+    ("Twc20", "p", 6, 4),
     ("ewc00", "s", -1, -1),
+    ("Twc30", "p", 7, 0),
     ("ewc10", "v", -1, -1),
-    ("Twc01", "p", 6, -1),
-    ("Lx3", "q", -1, -1),
-    ("Twc11", "p", 7, -1),
-    ("ewc01", "s", -1, -1),
-    ("ewc11", "v", -1, -1),
-    ("Twc20", "p", 0, 4),
-    ("Twc30", "p", 1, 0),
-    ("qwc0", "v", -1, -1),
     ("ewc20", "s", -1, -1),
-    ("qwc1", "v", -1, -1),
+    ("ewc30", "v", -1, -1),
+    ("Twc01", "p", 0, -1),
+    ("Twc11", "p", 1, -1),
     ("Twc21", "p", 2, -1),
-    ("ewc30", "s", -1, -1),
+    ("ewc01", "s", -1, -1),
     ("Twc31", "p", 3, -1),
+    ("ewc11", "v", -1, -1),
     ("ewc21", "s", -1, -1),
-    ("ewc31", "v", -1, -1),
-    ("qwc2", "v", -1, -1),
-    ("qwc3", "v", -1, -1),
+    ("qwc0", "v", -1, -1),
+    ("ewc31", "s", -1, -1),
+    ("qwc1", "v", -1, -1),
     ("Twb000", "p", 4, 1),
+    ("qwc2", "v", -1, -1),
     ("Twb001", "p", 5, -1),
+    ("Twb010", "p", 6, 2),
+    ("qwc3", "v", -1, -1),
     ("ewb000", "s", -1, -1),
-    ("M100", "p", 6, -1),
+    ("Twb011", "p", 7, -1),
     ("ewb001", "v", -1, -1),
+    ("ewb010", "s", -1, -1),
+    ("M100", "p", 0, -1),
     ("qwb00", "v", -1, -1),
-    ("M101", "p", 7, -1),
-    ("kve00", "s", -1, -1),
-    ("qkv00", "v", -1, -1),
-    ("Twb010", "p", 0, 2),
-    ("kve01", "s", -1, -1),
-    ("Twb011", "p", 1, -1),
-    ("ewb010", "v", -1, -1),
-    ("Twb020", "p", 2, 3),
     ("ewb011", "s", -1, -1),
-    ("Twb021", "p", 3, -1),
-    ("qkv01", "v", -1, -1),
-    ("Twb030", "p", 4, 4),
-    ("ewb020", "v", -1, -1),
-    ("ewb021", "s", -1, -1),
-    ("Twb031", "p", 5, -1),
     ("qwb01", "v", -1, -1),
-    ("M20000", "p", 6, -1),
-    ("ewb030", "s", -1, -1),
-    ("M20100", "p", 7, -1),
-    ("qwb02", "v", -1, -1),
-    ("M20001", "p", 0, -1),
-    ("ewb031", "s", -1, -1),
-    ("M20101", "p", 1, -1),
-    ("Twb100", "p", 2, 0),
+    ("M101", "p", 1, -1),
+    ("kve00", "s", -1, -1),
+    ("Twb020", "p", 2, 3),
+    ("qkv00", "v", -1, -1),
+    ("M20000", "p", 3, -1),
+    ("kve01", "s", -1, -1),
+    ("M20001", "p", 4, -1),
+    ("ewb020", "v", -1, -1),
+    ("Twb021", "p", 5, -1),
     ("o0000", "s", -1, -1),
-    ("qwb03", "v", -1, -1),
-    ("M20002", "p", 3, -1),
-    ("o0100", "s", -1, -1),
-    ("ewb100", "v", -1, -1),
-    ("M20102", "p", 4, -1),
-    ("M20003", "p", 5, -1),
+    ("qkv01", "v", -1, -1),
+    ("Twb030", "p", 6, 4),
+    ("M20100", "p", 7, -1),
     ("o0001", "s", -1, -1),
-    ("M20103", "p", 6, -1),
-    ("Twb101", "p", 7, -1),
-    ("o0101", "s", -1, -1),
+    ("ewb021", "v", -1, -1),
+    ("M20101", "p", 0, -1),
+    ("ewb030", "s", -1, -1),
+    ("Twb031", "p", 1, -1),
+    ("qwb02", "v", -1, -1),
+    ("Twb100", "p", 2, 0),
+    ("o0100", "s", -1, -1),
     ("mx000", "v", -1, -1),
-    ("Twb110", "p", 2, 1),
+    ("Twb101", "p", 3, -1),
+    ("o0101", "s", -1, -1),
+    ("M20002", "p", 4, -1),
+    ("M20102", "p", 5, -1),
+    ("ewb031", "s", -1, -1),
+    ("ewb100", "v", -1, -1),
+    ("Twb110", "p", 6, 1),
     ("o0002", "s", -1, -1),
-    ("Tx10", "p", 0, 2),
-    ("Tx11", "p", 1, -1),
-    ("o0102", "s", -1, -1),
+    ("Twb111", "p", 7, -1),
     ("mx010", "v", -1, -1),
-    ("Tx12", "p", 3, 3),
-    ("o0003", "s", -1, -1),
-    ("Tx13", "p", 4, -1),
-    ("o0103", "s", -1, -1),
-    ("ex10", "v", -1, -1),
-    ("Twb111", "p", 5, -1),
-    ("ex11", "s", -1, -1),
-    ("mx001", "v", -1, -1),
-    ("Twb120", "p", 6, 4),
-    ("Twb121", "p", 0, -1),
-    ("ex12", "s", -1, -1),
-    ("ex13", "s", -1, -1),
-    ("mx011", "v", -1, -1),
+    ("Twb120", "p", 0, 2),
+    ("o0102", "s", -1, -1),
+    ("Twb121", "p", 1, -1),
+    ("Twb130", "p", 2, 3),
     ("ewb101", "s", -1, -1),
-    ("ewb110", "s", -1, -1),
-    ("E10", "v", -1, -1),
-    ("qx10", "v", -1, -1),
-    ("ET0", "p", 1, -1),
-    ("ewb111", "s", -1, -1),
-    ("E20", "v", -1, -1),
-    ("Twb130", "p", 3, 2),
-    ("ewb120", "s", -1, -1),
+    ("qwb03", "v", -1, -1),
     ("Twb131", "p", 4, -1),
-    ("qx11", "v", -1, -1),
-    ("mu000", "g", -1, -1),
-    ("ewb121", "s", -1, -1),
+    ("ewb110", "s", -1, -1),
+    ("ewb111", "v", -1, -1),
+    ("Tx10", "p", 5, 4),
+    ("ewb120", "s", -1, -1),
+    ("Tx11", "p", 3, -1),
     ("qwb10", "v", -1, -1),
-    ("M110", "p", 7, -1),
-    ("ewb130", "s", -1, -1),
+    ("M20003", "p", 6, -1),
+    ("ex10", "s", -1, -1),
+    ("M20103", "p", 7, -1),
     ("qwb11", "v", -1, -1),
-    ("ewb131", "s", -1, -1),
-    ("qwb12", "v", -1, -1),
-    ("M111", "p", 2, -1),
-    ("mu001", "g", -1, -1),
-    ("kve10", "s", -1, -1),
-    ("qwb13", "v", -1, -1),
-    ("Sk000", "q", -1, -1),
-    ("qkv10", "v", -1, -1),
-    ("M20010", "p", 5, -1),
+    ("Tx12", "p", 0, 0),
+    ("ex11", "s", -1, -1),
+    ("ewb121", "v", -1, -1),
+    ("Tx13", "p", 5, -1),
+    ("o0003", "s", -1, -1),
+    ("M20010", "p", 3, -1),
+    ("qx10", "v", -1, -1),
     ("M20110", "p", 1, -1),
-    ("kve11", "s", -1, -1),
+    ("ex12", "s", -1, -1),
     ("M20011", "p", 6, -1),
-    ("o0010", "v", -1, -1),
+    ("ex13", "v", -1, -1),
+    ("o0103", "s", -1, -1),
     ("M20111", "p", 0, -1),
+    ("qx11", "v", -1, -1),
+    ("Tx20", "p", 5, 1),
+    ("o0010", "s", -1, -1),
+    ("Tx21", "p", 7, -1),
+    ("mx001", "v", -1, -1),
     ("o0110", "s", -1, -1),
-    ("M20012", "p", 3, -1),
-    ("qkv11", "v", -1, -1),
-    ("mu010", "g", -1, -1),
-    ("Sk001", "q", -1, -1),
-    ("o0011", "v", -1, -1),
-    ("M20112", "p", 4, -1),
+    ("M110", "p", 3, -1),
+    ("o0011", "s", -1, -1),
+    ("mx011", "v", -1, -1),
     ("o0111", "s", -1, -1),
-    ("M20013", "p", 7, -1),
-    ("o0012", "v", -1, -1),
-    ("M20113", "p", 2, -1),
     ("Sv000", "q", -1, -1),
-    ("o0112", "s", -1, -1),
+    ("M111", "p", 1, -1),
+    ("ewb130", "s", -1, -1),
     ("Sv010", "q", -1, -1),
-    ("M21000", "p", 5, -1),
-    ("o0013", "v", -1, -1),
-    ("M21001", "p", 1, -1),
-    ("o0113", "s", -1, -1),
-    ("M21002", "p", 6, -1),
-    ("M21003", "p", 0, -1),
-    ("Sv001", "q", -1, -1),
-    ("o1000", "s", -1, -1),
-    ("Sv011", "q", -1, -1),
-    ("M21100", "p", 3, -1),
-    ("mu011", "g", -1, -1),
-    ("Sk010", "q", -1, -1),
-    ("M21101", "p", 4, -1),
-    ("o1001", "s", -1, -1),
-    ("M21102", "p", 7, -1),
-    ("M21103", "p", 2, -1),
-    ("o1002", "s", -1, -1),
-    ("mx100", "v", -1, -1),
-    ("Tx20", "p", 5, 3),
-    ("o1003", "s", -1, -1),
-    ("Tx21", "p", 1, -1),
-    ("Tx22", "p", 6, 0),
-    ("o1100", "s", -1, -1),
-    ("ex20", "v", -1, -1),
-    ("Tx23", "p", 0, -1),
-    ("Sk011", "q", -1, -1),
-    ("o1101", "s", -1, -1),
-    ("mx101", "v", -1, -1),
-    ("M21010", "p", 3, -1),
-    ("M21011", "p", 5, -1),
-    ("o1102", "s", -1, -1),
-    ("M21012", "p", 4, -1),
-    ("o1103", "s", -1, -1),
-    ("mx110", "v", -1, -1),
-    ("M21013", "p", 7, -1),
+    ("E10", "v", -1, -1),
+    ("kve10", "v", -1, -1),
+    ("ewb131", "s", -1, -1),
+    ("ET0", "p", 6, -1),
+    ("qkv10", "v", -1, -1),
+    ("ex20", "s", -1, -1),
+    ("Tx22", "p", 0, 4),
+    ("qwb12", "v", -1, -1),
+    ("M21010", "p", 2, -1),
+    ("kve11", "s", -1, -1),
+    ("E20", "v", -1, -1),
+    ("M21011", "p", 3, -1),
+    ("M20012", "p", 4, -1),
     ("ex21", "s", -1, -1),
-    ("M21110", "p", 2, -1),
-    ("ex22", "s", -1, -1),
-    ("mx111", "v", -1, -1),
-    ("M21111", "p", 1, -1),
-    ("ex23", "s", -1, -1),
-    ("M21112", "p", 6, -1),
+    ("qkv11", "v", -1, -1),
+    ("M20112", "p", 5, -1),
+    ("qwb13", "v", -1, -1),
+    ("M21012", "p", 1, -1),
     ("o1010", "s", -1, -1),
-    ("E11", "v", -1, -1),
-    ("M21113", "p", 0, -1),
-    ("qx20", "v", -1, -1),
-    ("o1011", "s", -1, -1),
-    ("ET1", "p", 3, -1),
-    ("qx21", "v", -1, -1),
+    ("M21110", "p", 6, -1),
+    ("o0012", "v", -1, -1),
+    ("mu000", "g", -1, -1),
+    ("M21111", "p", 7, -1),
+    ("o0112", "s", -1, -1),
+    ("M20013", "p", 2, -1),
+    ("o1011", "v", -1, -1),
+    ("M20113", "p", 4, -1),
     ("o1012", "s", -1, -1),
-    ("Tx30", "p", 5, 1),
-    ("Sv100", "q", -1, -1),
-    ("E21", "v", -1, -1),
-    ("o1013", "s", -1, -1),
-    ("M120", "p", 4, -1),
+    ("M21013", "p", 5, -1),
+    ("mu001", "g", -1, -1),
     ("o1110", "v", -1, -1),
-    ("mu100", "g", -1, -1),
-    ("o1111", "s", -1, -1),
+    ("M21112", "p", 3, -1),
+    ("o0013", "s", -1, -1),
+    ("Sv100", "q", -1, -1),
+    ("M21113", "p", 1, -1),
+    ("o0113", "v", -1, -1),
+    ("Tx23", "p", 6, -1),
+    ("o1013", "s", -1, -1),
+    ("Sv001", "q", -1, -1),
+    ("mu002", "g", -1, -1),
+    ("M21000", "p", 2, -1),
+    ("o1111", "v", -1, -1),
+    ("Sk000p", "q", -1, -1),
+    ("o1112", "s", -1, -1),
+    ("Sv011", "q", -1, -1),
     ("Sv101", "q", -1, -1),
-    ("o1112", "v", -1, -1),
-    ("o1113", "s", -1, -1),
+    ("M21001", "p", 4, -1),
+    ("o1113", "v", -1, -1),
+    ("M21002", "p", 5, -1),
+    ("ex22", "s", -1, -1),
     ("Sv110", "q", -1, -1),
-    ("M121", "p", 3, -1),
-    ("ex30", "v", -1, -1),
-    ("kve20", "s", -1, -1),
+    ("M21003", "p", 7, -1),
+    ("mu003", "g", -1, -1),
+    ("ex23", "v", -1, -1),
+    ("M21100", "p", 3, -1),
+    ("o1000", "s", -1, -1),
     ("Sv111", "q", -1, -1),
-    ("qkv20", "v", -1, -1),
-    ("mu101", "g", -1, -1),
-    ("Tx31", "p", 7, -1),
-    ("Sk100", "q", -1, -1),
-    ("kve21", "s", -1, -1),
-    ("M22000", "p", 2, -1),
-    ("ex31", "v", -1, -1),
-    ("M22001", "p", 1, -1),
-    ("M22002", "p", 6, -1),
-    ("o2000", "s", -1, -1),
-    ("qkv21", "v", -1, -1),
-    ("M22003", "p", 0, -1),
-    ("qx30", "v", -1, -1),
-    ("M22100", "p", 5, -1),
-    ("o2001", "s", -1, -1),
-    ("M22101", "p", 4, -1),
-    ("mu110", "g", -1, -1),
-    ("M22102", "p", 3, -1),
-    ("Sk101", "q", -1, -1),
-    ("o2002", "s", -1, -1),
-    ("mx200", "v", -1, -1),
-    ("M22103", "p", 7, -1),
-    ("Tx32", "p", 2, 4),
-    ("o2003", "s", -1, -1),
+    ("M21101", "p", 1, -1),
+    ("M21102", "p", 0, -1),
+    ("o1001", "s", -1, -1),
+    ("M21103", "p", 6, -1),
+    ("qx20", "v", -1, -1),
+    ("Sk001p", "q", -1, -1),
+    ("Tx30", "p", 2, 0),
+    ("o1002", "s", -1, -1),
+    ("qx21", "v", -1, -1),
+    ("Tx31", "p", 4, -1),
+    ("o1003", "s", -1, -1),
+    ("Tx32", "p", 5, 2),
+    ("mx100", "v", -1, -1),
+    ("mu010", "g", -1, -1),
+    ("o1100", "s", -1, -1),
+    ("M120", "p", 7, -1),
+    ("o1101", "s", -1, -1),
+    ("mu011", "g", -1, -1),
+    ("mx101", "v", -1, -1),
+    ("o1102", "s", -1, -1),
+    ("M121", "p", 3, -1),
+    ("o1103", "s", -1, -1),
+    ("mu012", "g", -1, -1),
+    ("mx110", "v", -1, -1),
+    ("Sk010p", "q", -1, -1),
+    ("kve20", "s", -1, -1),
     ("Tx33", "p", 1, -1),
+    ("ex30", "s", -1, -1),
+    ("mu013", "g", -1, -1),
+    ("mx111", "v", -1, -1),
+    ("kve21", "s", -1, -1),
+    ("ex31", "s", -1, -1),
+    ("E11", "v", -1, -1),
+    ("Sk011p", "q", -1, -1),
+    ("qkv20", "v", -1, -1),
+    ("ex32", "s", -1, -1),
+    ("qkv21", "v", -1, -1),
+    ("ET1", "p", 0, -1),
+    ("qx30", "v", -1, -1),
+    ("M22010", "p", 6, -1),
+    ("ex33", "s", -1, -1),
+    ("M22011", "p", 7, -1),
+    ("E21", "v", -1, -1),
+    ("M22012", "p", 2, -1),
+    ("o2010", "s", -1, -1),
+    ("M22013", "p", 3, -1),
+    ("o2011", "v", -1, -1),
+    ("M22110", "p", 4, -1),
+    ("mu100", "g", -1, -1),
+    ("o2012", "s", -1, -1),
+    ("M22111", "p", 5, -1),
+    ("o2013", "v", -1, -1),
+    ("M22112", "p", 1, -1),
+    ("Sv200", "q", -1, -1),
+    ("o2110", "s", -1, -1),
+    ("M22113", "p", 0, -1),
+    ("o2111", "v", -1, -1),
+    ("M22000", "p", 6, -1),
+    ("mu101", "g", -1, -1),
+    ("Sv201", "q", -1, -1),
+    ("o2112", "s", -1, -1),
+    ("M22001", "p", 7, -1),
+    ("o2113", "v", -1, -1),
+    ("M22002", "p", 2, -1),
+    ("Sv210", "q", -1, -1),
+    ("o2000", "s", -1, -1),
+    ("M22003", "p", 3, -1),
+    ("M22100", "p", 4, -1),
+    ("qx31", "v", -1, -1),
+    ("Sv211", "q", -1, -1),
+    ("o2001", "s", -1, -1),
+    ("M22101", "p", 5, -1),
+    ("Sk100p", "q", -1, -1),
+    ("M22102", "p", 1, -1),
+    ("mu102", "g", -1, -1),
+    ("o2002", "s", -1, -1),
+    ("M22103", "p", 0, -1),
+    ("mx200", "v", -1, -1),
+    ("M130", "p", 6, -1),
+    ("o2003", "s", -1, -1),
+    ("mu103", "g", -1, -1),
     ("o2100", "s", -1, -1),
     ("mx201", "v", -1, -1),
-    ("M22010", "p", 6, -1),
-    ("M22011", "p", 0, -1),
+    ("M131", "p", 7, -1),
     ("o2101", "s", -1, -1),
-    ("M22012", "p", 5, -1),
-    ("mu111", "g", -1, -1),
-    ("Sk110", "q", -1, -1),
-    ("o2102", "s", -1, -1),
-    ("ex32", "v", -1, -1),
-    ("M22013", "p", 4, -1),
-    ("o2103", "s", -1, -1),
-    ("mx210", "v", -1, -1),
-    ("M22110", "p", 3, -1),
-    ("M22111", "p", 2, -1),
-    ("ex33", "s", -1, -1),
-    ("M22112", "p", 7, -1),
-    ("o2010", "s", -1, -1),
-    ("mx211", "v", -1, -1),
-    ("M22113", "p", 1, -1),
-    ("Sk111", "q", -1, -1),
-    ("o2011", "s", -1, -1),
-    ("o2012", "s", -1, -1),
-    ("E12", "v", -1, -1),
-    ("Sv200", "q", -1, -1),
-    ("qx31", "v", -1, -1),
-    ("ET2", "p", 6, -1),
-    ("o2013", "s", -1, -1),
-    ("o2110", "v", -1, -1),
-    ("M130", "p", 0, -1),
-    ("o2111", "s", -1, -1),
-    ("Sv201", "q", -1, -1),
-    ("E22", "v", -1, -1),
-    ("o2112", "s", -1, -1),
-    ("Sv210", "q", -1, -1),
-    ("o2113", "v", -1, -1),
-    ("mu200", "g", -1, -1),
-    ("M131", "p", 5, -1),
+    ("mu110", "g", -1, -1),
     ("kve30", "s", -1, -1),
-    ("Sv211", "q", -1, -1),
-    ("qkv30", "v", -1, -1),
-    ("M23000", "p", 4, -1),
-    ("M23001", "p", 3, -1),
+    ("Sk101p", "q", -1, -1),
+    ("mx210", "v", -1, -1),
+    ("o2102", "s", -1, -1),
+    ("mu111", "g", -1, -1),
     ("kve31", "s", -1, -1),
-    ("M23002", "p", 2, -1),
-    ("mu201", "g", -1, -1),
-    ("M23003", "p", 6, -1),
-    ("Sk200", "q", -1, -1),
-    ("o3000", "s", -1, -1),
+    ("o2103", "s", -1, -1),
+    ("qkv30", "v", -1, -1),
     ("qkv31", "v", -1, -1),
-    ("M23010", "p", 7, -1),
-    ("M23100", "p", 1, -1),
-    ("o3001", "s", -1, -1),
-    ("M23101", "p", 0, -1),
-    ("o3010", "v", -1, -1),
-    ("M23102", "p", 5, -1),
-    ("o3002", "s", -1, -1),
-    ("M23103", "p", 4, -1),
-    ("mx300", "v", -1, -1),
+    ("Sk110p", "q", -1, -1),
+    ("mu112", "g", -1, -1),
+    ("M23010", "p", 2, -1),
+    ("mx211", "v", -1, -1),
     ("M23011", "p", 3, -1),
-    ("o3003", "s", -1, -1),
-    ("M23012", "p", 7, -1),
-    ("mu210", "g", -1, -1),
-    ("Sk201", "q", -1, -1),
-    ("M23013", "p", 2, -1),
-    ("o3100", "s", -1, -1),
+    ("M23012", "p", 4, -1),
+    ("o3010", "s", -1, -1),
+    ("M23013", "p", 5, -1),
+    ("mu113", "g", -1, -1),
     ("M23110", "p", 6, -1),
+    ("E12", "v", -1, -1),
+    ("o3011", "s", -1, -1),
+    ("M23111", "p", 1, -1),
+    ("o3012", "v", -1, -1),
+    ("ET2", "p", 7, -1),
+    ("M23112", "p", 0, -1),
+    ("o3013", "s", -1, -1),
+    ("o3110", "v", -1, -1),
+    ("Sv300", "q", -1, -1),
+    ("M23113", "p", 2, -1),
+    ("Sk111p", "q", -1, -1),
+    ("o3111", "s", -1, -1),
+    ("M23000", "p", 3, -1),
+    ("E22", "v", -1, -1),
+    ("Sv301", "q", -1, -1),
+    ("M23001", "p", 4, -1),
+    ("o3112", "s", -1, -1),
+    ("M23002", "p", 5, -1),
+    ("o3113", "v", -1, -1),
+    ("Sv310", "q", -1, -1),
+    ("M23003", "p", 6, -1),
+    ("mu200", "g", -1, -1),
+    ("o3000", "s", -1, -1),
+    ("M23100", "p", 1, -1),
+    ("M23101", "p", 7, -1),
+    ("Sv311", "q", -1, -1),
+    ("o3001", "s", -1, -1),
+    ("M23102", "p", 0, -1),
+    ("mu201", "g", -1, -1),
+    ("M23103", "p", 2, -1),
+    ("o3002", "s", -1, -1),
+    ("mx300", "v", -1, -1),
+    ("o3003", "s", -1, -1),
+    ("mu202", "g", -1, -1),
+    ("Sk200p", "q", -1, -1),
+    ("o3100", "s", -1, -1),
     ("mx301", "v", -1, -1),
     ("o3101", "s", -1, -1),
-    ("M23111", "p", 1, -1),
+    ("mu203", "g", -1, -1),
     ("o3102", "s", -1, -1),
-    ("M23112", "p", 0, -1),
     ("mx310", "v", -1, -1),
     ("o3103", "s", -1, -1),
-    ("M23113", "p", 5, -1),
-    ("mu211", "g", -1, -1),
-    ("Sk210", "q", -1, -1),
-    ("o3011", "s", -1, -1),
+    ("mu210", "g", -1, -1),
+    ("Sk201p", "q", -1, -1),
     ("mx311", "v", -1, -1),
-    ("o3012", "s", -1, -1),
-    ("Sv300", "q", -1, -1),
-    ("o3013", "s", -1, -1),
+    ("mu211", "g", -1, -1),
     ("E13", "v", -1, -1),
-    ("o3110", "v", -1, -1),
-    ("ET3", "p", 4, -1),
-    ("o3111", "s", -1, -1),
-    ("Sv301", "q", -1, -1),
-    ("Sk211", "q", -1, -1),
-    ("o3112", "v", -1, -1),
-    ("o3113", "s", -1, -1),
-    ("Sv310", "q", -1, -1),
+    ("ET3", "p", 3, -1),
+    ("mu212", "g", -1, -1),
+    ("Sk210p", "q", -1, -1),
     ("E23", "v", -1, -1),
-    ("Sv311", "q", -1, -1),
+    ("mu213", "g", -1, -1),
     ("mu300", "v", -1, -1),
     ("mu303", "s", -1, -1),
-    ("mu301", "g", -1, -1),
     ("mu302", "v", -1, -1),
-    ("Sk300", "q", -1, -1),
-    ("mu313", "s", -1, -1),
+    ("mu301", "g", -1, -1),
     ("mu310", "v", -1, -1),
-    ("mu311", "g", -1, -1),
-    ("Sk303", "q", -1, -1),
-    ("Sk301", "q", -1, -1),
-    ("Sk302", "q", -1, -1),
+    ("Sk211p", "q", -1, -1),
+    ("mu313", "s", -1, -1),
+    ("Sk301p", "q", -1, -1),
     ("mu312", "v", -1, -1),
-    ("Sk310", "q", -1, -1),
-    ("Sk311", "q", -1, -1),
-    ("Sk312", "q", -1, -1),
-    ("Sk313", "q", -1, -1),
+    ("mu311", "g", -1, -1),
+    ("Sk300p", "q", -1, -1),
+    ("Sk311p", "q", -1, -1),
+    ("Sk310p", "q", -1, -1),
 ]
 
 
@@ -425,18 +430,11 @@ def tile_ssa_pb_kernel(tc, x, wkv_c, wkv_b, out_0, out_1):
             if name[0] == "x":
                 b = int(name[1])
                 t = slab("x%d" % b, [P, 2, D], BF16)
-                if b == 0:
-                    half = 0 if name[2] == "a" else 1
-                    cols = slice(1024 * half, 1024 * half + 1024)
-                    nc.sync.dma_start(out=t[:, :, cols], in_=x_view[b, :, :, cols])
-                else:
-                    nc.sync.dma_start(out=t[:], in_=x_view[b])
+                nc.sync.dma_start(out=t[:], in_=x_view[b])
             elif name[:2] == "wc":
-                half, u = int(name[2]), int(name[3])
-                t = slab("wc%d" % half, [P, 2, 2, 1024], BF16)
-                nc.sync.dma_start(
-                    out=t[:, u], in_=wc_view[u, :, :, 1024 * half : 1024 * half + 1024]
-                )
+                u = int(name[2])
+                t = slab(name, [P, 2, D], BF16)
+                nc.sync.dma_start(out=t[:], in_=wc_view[u])
             else:
                 v, half = int(name[2]), int(name[3])
                 t = slab(name, [P, 8, KVL], BF16)
@@ -464,7 +462,7 @@ def tile_ssa_pb_kernel(tc, x, wkv_c, wkv_b, out_0, out_1):
             if name[:2] == "wc":
                 g, u = int(name[2]), int(name[3])
                 return [
-                    words(live["wc%d" % (g // 2)][:, u, e, :], 256 * (g % 2) + P * u2)
+                    words(live["wc%d" % u][:, e, :], 256 * g + P * u2)
                     for e in range(2)
                     for u2 in range(2)
                 ]
@@ -624,8 +622,8 @@ def tile_ssa_pb_kernel(tc, x, wkv_c, wkv_b, out_0, out_1):
                         scale=eta[:, h : h + 1],
                     )
 
-        def store_keys(b, r, k):
-            n = H // len(MUL[b])
+        def store_keys(b, r, k, pieces):
+            n = pieces * H // len(MUL[b])
             cols = slice(P * n * k, P * n * (k + 1))
             nc.sync.dma_start(out=k_view[b, r, :, cols], in_=live["a%d%d" % (b, r)][:, cols])
 
@@ -667,4 +665,4 @@ def tile_ssa_pb_kernel(tc, x, wkv_c, wkv_b, out_0, out_1):
                 scale_heads(d[0], d[1], d[2], engine)
             else:
                 assert name[:2] == "Sk"
-                store_keys(d[0], d[1], d[2])
+                store_keys(d[0], d[1], d[2], 2 if name[-1] == "p" else 1)

@@ -16,372 +16,33 @@ P = 128
 B, S, D, H, KVL = 4, 256, 2048, 16, 512
 G = D // 512
 FLOPS = 2 * B * S * D * KVL + 2 * B * S * KVL * H * 256
-NSLAB = 18
-MUL = ["GGGG","GGGG","GGGG","VGVS"]
 
-ORDER = [
-    ("Lx0", "q", -1, -1),
-    ("Lwc0", "q", -1, -1),
-    ("Lwc1", "q", -1, -1),
-    ("Lwb00", "q", -1, -1),
-    ("Lwb01", "q", -1, -1),
-    ("Lwb10", "q", -1, -1),
-    ("Lwb11", "q", -1, -1),
-    ("Lx1", "q", -1, -1),
-    ("Lx2", "q", -1, -1),
-    ("Lx3", "q", -1, -1),
-    ("Tx00", "p", 0, 0),
-    ("Tx01", "p", 1, -1),
-    ("Tx02", "p", 2, 1),
-    ("ex00", "s", -1, -1),
-    ("Tx03", "p", 3, -1),
-    ("ex01", "v", -1, -1),
-    ("ex02", "s", -1, -1),
-    ("qx00", "v", -1, -1),
-    ("ex03", "s", -1, -1),
-    ("Twc00", "p", 4, 2),
-    ("Twc10", "p", 5, 3),
-    ("qx01", "v", -1, -1),
-    ("Twc20", "p", 6, 4),
-    ("ewc00", "s", -1, -1),
-    ("Twc30", "p", 7, 0),
-    ("ewc10", "v", -1, -1),
-    ("ewc20", "s", -1, -1),
-    ("ewc30", "v", -1, -1),
-    ("Twc01", "p", 0, -1),
-    ("Twc11", "p", 1, -1),
-    ("Twc21", "p", 2, -1),
-    ("ewc01", "s", -1, -1),
-    ("Twc31", "p", 3, -1),
-    ("ewc11", "v", -1, -1),
-    ("ewc21", "s", -1, -1),
-    ("qwc0", "v", -1, -1),
-    ("ewc31", "s", -1, -1),
-    ("qwc1", "v", -1, -1),
-    ("Twb000", "p", 4, 1),
-    ("qwc2", "v", -1, -1),
-    ("Twb001", "p", 5, -1),
-    ("Twb010", "p", 6, 2),
-    ("qwc3", "v", -1, -1),
-    ("ewb000", "s", -1, -1),
-    ("Twb011", "p", 7, -1),
-    ("ewb001", "v", -1, -1),
-    ("ewb010", "s", -1, -1),
-    ("M100", "p", 0, -1),
-    ("qwb00", "v", -1, -1),
-    ("ewb011", "s", -1, -1),
-    ("qwb01", "v", -1, -1),
-    ("M101", "p", 1, -1),
-    ("kve00", "s", -1, -1),
-    ("Twb020", "p", 2, 3),
-    ("qkv00", "v", -1, -1),
-    ("M20000", "p", 3, -1),
-    ("kve01", "s", -1, -1),
-    ("M20001", "p", 4, -1),
-    ("ewb020", "v", -1, -1),
-    ("Twb021", "p", 5, -1),
-    ("o0000", "s", -1, -1),
-    ("qkv01", "v", -1, -1),
-    ("Twb030", "p", 6, 4),
-    ("M20100", "p", 7, -1),
-    ("o0001", "s", -1, -1),
-    ("ewb021", "v", -1, -1),
-    ("M20101", "p", 0, -1),
-    ("ewb030", "s", -1, -1),
-    ("Twb031", "p", 1, -1),
-    ("qwb02", "v", -1, -1),
-    ("Twb100", "p", 2, 0),
-    ("o0100", "s", -1, -1),
-    ("mx000", "v", -1, -1),
-    ("Twb101", "p", 3, -1),
-    ("o0101", "s", -1, -1),
-    ("M20002", "p", 4, -1),
-    ("M20102", "p", 5, -1),
-    ("ewb031", "s", -1, -1),
-    ("ewb100", "v", -1, -1),
-    ("Twb110", "p", 6, 1),
-    ("o0002", "s", -1, -1),
-    ("Twb111", "p", 7, -1),
-    ("mx010", "v", -1, -1),
-    ("Twb120", "p", 0, 2),
-    ("o0102", "s", -1, -1),
-    ("Twb121", "p", 1, -1),
-    ("Twb130", "p", 2, 3),
-    ("ewb101", "s", -1, -1),
-    ("qwb03", "v", -1, -1),
-    ("Twb131", "p", 4, -1),
-    ("ewb110", "s", -1, -1),
-    ("ewb111", "v", -1, -1),
-    ("Tx10", "p", 5, 4),
-    ("ewb120", "s", -1, -1),
-    ("Tx11", "p", 3, -1),
-    ("qwb10", "v", -1, -1),
-    ("M20003", "p", 6, -1),
-    ("ex10", "s", -1, -1),
-    ("M20103", "p", 7, -1),
-    ("qwb11", "v", -1, -1),
-    ("Tx12", "p", 0, 0),
-    ("ex11", "s", -1, -1),
-    ("ewb121", "v", -1, -1),
-    ("Tx13", "p", 5, -1),
-    ("o0003", "s", -1, -1),
-    ("M20010", "p", 3, -1),
-    ("qx10", "v", -1, -1),
-    ("M20110", "p", 1, -1),
-    ("ex12", "s", -1, -1),
-    ("M20011", "p", 6, -1),
-    ("ex13", "v", -1, -1),
-    ("o0103", "s", -1, -1),
-    ("M20111", "p", 0, -1),
-    ("qx11", "v", -1, -1),
-    ("Tx20", "p", 5, 1),
-    ("o0010", "s", -1, -1),
-    ("Tx21", "p", 7, -1),
-    ("mx001", "v", -1, -1),
-    ("o0110", "s", -1, -1),
-    ("M110", "p", 3, -1),
-    ("o0011", "s", -1, -1),
-    ("mx011", "v", -1, -1),
-    ("o0111", "s", -1, -1),
-    ("Sv000", "q", -1, -1),
-    ("M111", "p", 1, -1),
-    ("ewb130", "s", -1, -1),
-    ("Sv010", "q", -1, -1),
-    ("E10", "v", -1, -1),
-    ("kve10", "v", -1, -1),
-    ("ewb131", "s", -1, -1),
-    ("ET0", "p", 6, -1),
-    ("qkv10", "v", -1, -1),
-    ("ex20", "s", -1, -1),
-    ("Tx22", "p", 0, 4),
-    ("qwb12", "v", -1, -1),
-    ("M21010", "p", 2, -1),
-    ("kve11", "s", -1, -1),
-    ("E20", "v", -1, -1),
-    ("M21011", "p", 3, -1),
-    ("M20012", "p", 4, -1),
-    ("ex21", "s", -1, -1),
-    ("qkv11", "v", -1, -1),
-    ("M20112", "p", 5, -1),
-    ("qwb13", "v", -1, -1),
-    ("M21012", "p", 1, -1),
-    ("o1010", "s", -1, -1),
-    ("M21110", "p", 6, -1),
-    ("o0012", "v", -1, -1),
-    ("mu000", "g", -1, -1),
-    ("M21111", "p", 7, -1),
-    ("o0112", "s", -1, -1),
-    ("M20013", "p", 2, -1),
-    ("o1011", "v", -1, -1),
-    ("M20113", "p", 4, -1),
-    ("o1012", "s", -1, -1),
-    ("M21013", "p", 5, -1),
-    ("mu001", "g", -1, -1),
-    ("o1110", "v", -1, -1),
-    ("M21112", "p", 3, -1),
-    ("o0013", "s", -1, -1),
-    ("Sv100", "q", -1, -1),
-    ("M21113", "p", 1, -1),
-    ("o0113", "v", -1, -1),
-    ("Tx23", "p", 6, -1),
-    ("o1013", "s", -1, -1),
-    ("Sv001", "q", -1, -1),
-    ("mu002", "g", -1, -1),
-    ("M21000", "p", 2, -1),
-    ("o1111", "v", -1, -1),
-    ("Sk000p", "q", -1, -1),
-    ("o1112", "s", -1, -1),
-    ("Sv011", "q", -1, -1),
-    ("Sv101", "q", -1, -1),
-    ("M21001", "p", 4, -1),
-    ("o1113", "v", -1, -1),
-    ("M21002", "p", 5, -1),
-    ("ex22", "s", -1, -1),
-    ("Sv110", "q", -1, -1),
-    ("M21003", "p", 7, -1),
-    ("mu003", "g", -1, -1),
-    ("ex23", "v", -1, -1),
-    ("M21100", "p", 3, -1),
-    ("o1000", "s", -1, -1),
-    ("Sv111", "q", -1, -1),
-    ("M21101", "p", 1, -1),
-    ("M21102", "p", 0, -1),
-    ("o1001", "s", -1, -1),
-    ("M21103", "p", 6, -1),
-    ("qx20", "v", -1, -1),
-    ("Sk001p", "q", -1, -1),
-    ("Tx30", "p", 2, 0),
-    ("o1002", "s", -1, -1),
-    ("qx21", "v", -1, -1),
-    ("Tx31", "p", 4, -1),
-    ("o1003", "s", -1, -1),
-    ("Tx32", "p", 5, 2),
-    ("mx100", "v", -1, -1),
-    ("mu010", "g", -1, -1),
-    ("o1100", "s", -1, -1),
-    ("M120", "p", 7, -1),
-    ("o1101", "s", -1, -1),
-    ("mu011", "g", -1, -1),
-    ("mx101", "v", -1, -1),
-    ("o1102", "s", -1, -1),
-    ("M121", "p", 3, -1),
-    ("o1103", "s", -1, -1),
-    ("mu012", "g", -1, -1),
-    ("mx110", "v", -1, -1),
-    ("Sk010p", "q", -1, -1),
-    ("kve20", "s", -1, -1),
-    ("Tx33", "p", 1, -1),
-    ("ex30", "s", -1, -1),
-    ("mu013", "g", -1, -1),
-    ("mx111", "v", -1, -1),
-    ("kve21", "s", -1, -1),
-    ("ex31", "s", -1, -1),
-    ("E11", "v", -1, -1),
-    ("Sk011p", "q", -1, -1),
-    ("qkv20", "v", -1, -1),
-    ("ex32", "s", -1, -1),
-    ("qkv21", "v", -1, -1),
-    ("ET1", "p", 0, -1),
-    ("qx30", "v", -1, -1),
-    ("M22010", "p", 6, -1),
-    ("ex33", "s", -1, -1),
-    ("M22011", "p", 7, -1),
-    ("E21", "v", -1, -1),
-    ("M22012", "p", 2, -1),
-    ("o2010", "s", -1, -1),
-    ("M22013", "p", 3, -1),
-    ("o2011", "v", -1, -1),
-    ("M22110", "p", 4, -1),
-    ("mu100", "g", -1, -1),
-    ("o2012", "s", -1, -1),
-    ("M22111", "p", 5, -1),
-    ("o2013", "v", -1, -1),
-    ("M22112", "p", 1, -1),
-    ("Sv200", "q", -1, -1),
-    ("o2110", "s", -1, -1),
-    ("M22113", "p", 0, -1),
-    ("o2111", "v", -1, -1),
-    ("M22000", "p", 6, -1),
-    ("mu101", "g", -1, -1),
-    ("Sv201", "q", -1, -1),
-    ("o2112", "s", -1, -1),
-    ("M22001", "p", 7, -1),
-    ("o2113", "v", -1, -1),
-    ("M22002", "p", 2, -1),
-    ("Sv210", "q", -1, -1),
-    ("o2000", "s", -1, -1),
-    ("M22003", "p", 3, -1),
-    ("M22100", "p", 4, -1),
-    ("qx31", "v", -1, -1),
-    ("Sv211", "q", -1, -1),
-    ("o2001", "s", -1, -1),
-    ("M22101", "p", 5, -1),
-    ("Sk100p", "q", -1, -1),
-    ("M22102", "p", 1, -1),
-    ("mu102", "g", -1, -1),
-    ("o2002", "s", -1, -1),
-    ("M22103", "p", 0, -1),
-    ("mx200", "v", -1, -1),
-    ("M130", "p", 6, -1),
-    ("o2003", "s", -1, -1),
-    ("mu103", "g", -1, -1),
-    ("o2100", "s", -1, -1),
-    ("mx201", "v", -1, -1),
-    ("M131", "p", 7, -1),
-    ("o2101", "s", -1, -1),
-    ("mu110", "g", -1, -1),
-    ("kve30", "s", -1, -1),
-    ("Sk101p", "q", -1, -1),
-    ("mx210", "v", -1, -1),
-    ("o2102", "s", -1, -1),
-    ("mu111", "g", -1, -1),
-    ("kve31", "s", -1, -1),
-    ("o2103", "s", -1, -1),
-    ("qkv30", "v", -1, -1),
-    ("qkv31", "v", -1, -1),
-    ("Sk110p", "q", -1, -1),
-    ("mu112", "g", -1, -1),
-    ("M23010", "p", 2, -1),
-    ("mx211", "v", -1, -1),
-    ("M23011", "p", 3, -1),
-    ("M23012", "p", 4, -1),
-    ("o3010", "s", -1, -1),
-    ("M23013", "p", 5, -1),
-    ("mu113", "g", -1, -1),
-    ("M23110", "p", 6, -1),
-    ("E12", "v", -1, -1),
-    ("o3011", "s", -1, -1),
-    ("M23111", "p", 1, -1),
-    ("o3012", "v", -1, -1),
-    ("ET2", "p", 7, -1),
-    ("M23112", "p", 0, -1),
-    ("o3013", "s", -1, -1),
-    ("o3110", "v", -1, -1),
-    ("Sv300", "q", -1, -1),
-    ("M23113", "p", 2, -1),
-    ("Sk111p", "q", -1, -1),
-    ("o3111", "s", -1, -1),
-    ("M23000", "p", 3, -1),
-    ("E22", "v", -1, -1),
-    ("Sv301", "q", -1, -1),
-    ("M23001", "p", 4, -1),
-    ("o3112", "s", -1, -1),
-    ("M23002", "p", 5, -1),
-    ("o3113", "v", -1, -1),
-    ("Sv310", "q", -1, -1),
-    ("M23003", "p", 6, -1),
-    ("mu200", "g", -1, -1),
-    ("o3000", "s", -1, -1),
-    ("M23100", "p", 1, -1),
-    ("M23101", "p", 7, -1),
-    ("Sv311", "q", -1, -1),
-    ("o3001", "s", -1, -1),
-    ("M23102", "p", 0, -1),
-    ("mu201", "g", -1, -1),
-    ("M23103", "p", 2, -1),
-    ("o3002", "s", -1, -1),
-    ("mx300", "v", -1, -1),
-    ("o3003", "s", -1, -1),
-    ("mu202", "g", -1, -1),
-    ("Sk200p", "q", -1, -1),
-    ("o3100", "s", -1, -1),
-    ("mx301", "v", -1, -1),
-    ("o3101", "s", -1, -1),
-    ("mu203", "g", -1, -1),
-    ("o3102", "s", -1, -1),
-    ("mx310", "v", -1, -1),
-    ("o3103", "s", -1, -1),
-    ("mu210", "g", -1, -1),
-    ("Sk201p", "q", -1, -1),
-    ("mx311", "v", -1, -1),
-    ("mu211", "g", -1, -1),
-    ("E13", "v", -1, -1),
-    ("ET3", "p", 3, -1),
-    ("mu212", "g", -1, -1),
-    ("Sk210p", "q", -1, -1),
-    ("E23", "v", -1, -1),
-    ("mu213", "g", -1, -1),
-    ("mu300", "v", -1, -1),
-    ("mu303", "s", -1, -1),
-    ("mu302", "v", -1, -1),
-    ("mu301", "g", -1, -1),
-    ("mu310", "v", -1, -1),
-    ("Sk211p", "q", -1, -1),
-    ("mu313", "s", -1, -1),
-    ("Sk301p", "q", -1, -1),
-    ("mu312", "v", -1, -1),
-    ("mu311", "g", -1, -1),
-    ("Sk300p", "q", -1, -1),
-    ("Sk311p", "q", -1, -1),
-    ("Sk310p", "q", -1, -1),
-]
+BANKS = 8
+STAGES = 5
+SLABS = 18
+
+X0_OUT = "svsv"
+WC_OUT = "sssvsssv"
+WB_OUT = "svsv"
+X_OUT = "sssv"
+VALUES_OUT = "svssvssv"
+STAGE1_OUT = "ss"
+CLAMP = "gggv"
+CLAMP_LAST = "vgvs"
+LAG_QUANTISE = 3
+LAG_STAGE1_QUANTISE = 2
+LAG_MAX = 1
+LAG_STORE = 1
+LAG_FACTORS = 9
+LAG_KEY_STORE = 6
+STEP_KEY_STORE = 7
 
 
 def tile_ssa_pb_kernel(tc, x, wkv_c, wkv_b, out_0, out_1):
     nc = tc.nc
     with ExitStack() as ctx:
         const = ctx.enter_context(tc.tile_pool(name="const", bufs=1))
-        slabs = ctx.enter_context(tc.tile_pool(name="slabs", bufs=NSLAB))
+        slabs = ctx.enter_context(tc.tile_pool(name="slabs", bufs=SLABS))
         stage = ctx.enter_context(tc.tile_pool(name="stage", bufs=1))
         keep = ctx.enter_context(tc.tile_pool(name="keep", bufs=1))
         small = ctx.enter_context(tc.tile_pool(name="small", bufs=2))
@@ -393,6 +54,32 @@ def tile_ssa_pb_kernel(tc, x, wkv_c, wkv_b, out_0, out_1):
         wb_view = wkv_b.rearrange("(h v c) k -> v c h k", v=2, c=P)
         k_view = out_0.rearrange("b (p r) h d -> b r p (h d)", r=2)
         v_view = out_1.rearrange("b (p r) h d -> b r p (h d)", r=2)
+
+        x_sb, wc_sb, wb_sb = {}, {}, {}
+
+        def load_x(b):
+            x_sb[b] = slabs.tile([P, 2, D], BF16, name="x_sb%d" % b, tag="slab")
+            nc.sync.dma_start(out=x_sb[b][:], in_=x_view[b])
+
+        def load_wc(u):
+            wc_sb[u] = slabs.tile([P, 2, D], BF16, name="wc_sb%d" % u, tag="slab")
+            nc.sync.dma_start(out=wc_sb[u][:], in_=wc_view[u])
+
+        def load_wb(v, half):
+            t = slabs.tile([P, 8, KVL], BF16, name="wb_sb%d%d" % (v, half), tag="slab")
+            nc.sync.dma_start(out=t[:], in_=wb_view[v, :, 8 * half : 8 * half + 8, :])
+            wb_sb[(v, half)] = t
+
+        load_x(0)
+        load_wc(0)
+        load_wc(1)
+        load_wb(1, 0)
+        load_x(1)
+        load_wb(1, 1)
+        load_wb(0, 0)
+        load_wb(0, 1)
+        load_x(2)
+        load_x(3)
 
         ident = const.tile([P, P], F32, name="ident")
         make_identity(nc, ident[:])
@@ -409,140 +96,144 @@ def tile_ssa_pb_kernel(tc, x, wkv_c, wkv_b, out_0, out_1):
         kv_codes = keep.tile([P, B, S], U32, name="kv_codes", align_bytes=64)
         kv_scales = keep.tile([P, B, S], U8, name="kv_scales", align_bytes=64)
 
-        live = {}
+        count = {"job": 0, "bank": 0, "stage": 0}
+        waiting = {"list": []}
 
-        def slab(key, shape, dtype):
-            if key not in live:
-                live[key] = slabs.tile(shape, dtype, name="slab_" + key, tag="slab")
-            return live[key]
+        def later(lag, fn, *args):
+            waiting["list"].append((count["job"] + lag, fn, args))
 
-        def bank(key, ps, shape):
-            live[key] = psum.tile(shape, F32, name="bank_" + key, tag="ps%d" % ps)
-            return live[key]
+        def job_done():
+            count["job"] += 1
+            due = [w for w in waiting["list"] if w[0] <= count["job"]]
+            waiting["list"] = [w for w in waiting["list"] if w[0] > count["job"]]
+            for w in due:
+                w[1](*w[2])
 
-        def evac(engine, out, in_):
+        def next_bank(shape):
+            n = count["bank"]
+            count["bank"] += 1
+            return psum.tile(shape, F32, name="bank%d" % n, tag="bank%d" % (n % BANKS))
+
+        def empty(engine, out, in_):
             if engine == "v":
                 nc.vector.tensor_copy(out=out, in_=in_)
             else:
                 nc.scalar.copy(out=out, in_=in_)
 
-        def load(name):
-            if name[0] == "x":
-                b = int(name[1])
-                t = slab("x%d" % b, [P, 2, D], BF16)
-                nc.sync.dma_start(out=t[:], in_=x_view[b])
-            elif name[:2] == "wc":
-                u = int(name[2])
-                t = slab(name, [P, 2, D], BF16)
-                nc.sync.dma_start(out=t[:], in_=wc_view[u])
-            else:
-                v, half = int(name[2]), int(name[3])
-                t = slab(name, [P, 8, KVL], BF16)
-                nc.sync.dma_start(out=t[:], in_=wb_view[v, :, 8 * half : 8 * half + 8, :])
-
         def words(ap, first):
             return ap.bitcast(F32)[:, first : first + P]
 
-        def group_of(name):
-            if name[0] == "x":
-                g = int(name[2])
-                return "x%s%d" % (name[1], g // 2), g % 2
-            if name[:2] == "wc":
-                return name[:3], int(name[3])
-            return name[:4], int(name[4])
+        def quantise(grouped, codes, scales):
+            nc.vector.quantize_mx(out=codes.bitcast(FP8X4), scales=scales, in_=grouped[:])
 
-        def sources(name):
-            if name[0] == "x":
-                b, g = int(name[1]), int(name[2])
-                return [
-                    words(live["x%d" % b][:, r, :], 256 * g + P * u)
-                    for r in range(2)
-                    for u in range(2)
-                ]
-            if name[:2] == "wc":
-                g, u = int(name[2]), int(name[3])
-                return [
-                    words(live["wc%d" % u][:, e, :], 256 * g + P * u2)
-                    for e in range(2)
-                    for u2 in range(2)
-                ]
-            v, hq, pp = int(name[2]), int(name[3]), int(name[4])
-            srcs = []
-            for hh in range(2):
-                h = 4 * hq + 2 * pp + hh
-                for u in range(2):
-                    srcs.append(words(live["wb%d%d" % (v, h // 8)][:, h % 8, :], P * u))
-            return srcs
-
-        def flip(name, ps, grp):
-            key, half = group_of(name)
-            if half == 0:
-                live["g" + key] = stage.tile(
-                    [P, 2048], BF16, name="grp_" + key, tag="grp%d" % grp, align_bytes=64
+        def flips(banks, targets, engines):
+            grouped = None
+            for i in range(len(banks)):
+                if i % 2 == 0:
+                    n = count["stage"]
+                    count["stage"] += 1
+                    grouped = stage.tile(
+                        [P, 2048], BF16, name="grouped%d" % n, tag="stage%d" % (n % STAGES), align_bytes=64
+                    )
+                bank = next_bank([P, 4, P])
+                for j in range(4):
+                    nc.tensor.transpose(bank[:, j, :], banks[i][j], ident[:])
+                half = 2 * (i % 2)
+                empty(
+                    engines[i % len(engines)],
+                    grouped[:].bitcast(F32).rearrange("q (a c u) -> q a c u", a=4, u=2)[:, half : half + 2],
+                    bank[:].rearrange("q (a u) c -> q a c u", u=2),
                 )
-            t = bank("T" + name, ps, [P, 4, P])
-            srcs = sources(name)
-            for i in range(4):
-                nc.tensor.transpose(t[:, i, :], srcs[i], ident[:])
+                if i % 2 == 1:
+                    later(LAG_QUANTISE, quantise, grouped, targets[i // 2][0], targets[i // 2][1])
+                job_done()
 
-        def flip_out(name, engine):
-            key, half = group_of(name)
-            dst = live["g" + key][:].bitcast(F32).rearrange("q (a c u) -> q a c u", a=4, u=2)
-            evac(
-                engine,
-                dst[:, 2 * half : 2 * half + 2],
-                live["T" + name][:].rearrange("q (a u) c -> q a c u", u=2),
+        def flips_x(b, engines):
+            flips(
+                [
+                    [words(x_sb[b][:, r, :], 256 * g + P * u) for r in range(2) for u in range(2)]
+                    for g in range(G)
+                ],
+                [
+                    (
+                        x_codes[:, b, 2 * gp : 2 * gp + 2, :].rearrange("q g s -> q (g s)"),
+                        x_scales[:, b, 2 * gp : 2 * gp + 2, :].rearrange("q g s -> q (g s)"),
+                    )
+                    for gp in range(2)
+                ],
+                engines,
             )
 
-        def quantise(key):
-            if key[0] == "x":
-                b, gp = int(key[1]), int(key[2])
-                codes = x_codes[:, b, 2 * gp : 2 * gp + 2, :].rearrange("q g s -> q (g s)")
-                scales = x_scales[:, b, 2 * gp : 2 * gp + 2, :].rearrange("q g s -> q (g s)")
-            elif key[:2] == "wc":
-                g = int(key[2])
-                codes, scales = wc_codes[:, g, :], wc_scales[:, g, :]
-            else:
-                v, hq = int(key[2]), int(key[3])
-                cols = slice(512 * hq, 512 * hq + 512)
-                codes, scales = wb_codes[:, v, cols], wb_scales[:, v, cols]
-            nc.vector.quantize_mx(out=codes.bitcast(FP8X4), scales=scales, in_=live["g" + key][:])
+        def flips_wc():
+            flips(
+                [
+                    [words(wc_sb[u][:, e, :], 256 * g + P * u2) for e in range(2) for u2 in range(2)]
+                    for g in range(G)
+                    for u in range(2)
+                ],
+                [(wc_codes[:, g, :], wc_scales[:, g, :]) for g in range(G)],
+                WC_OUT,
+            )
 
-        def stage1(b, r, ps):
-            acc = bank("M1%d%d" % (b, r), ps, [P, 4, P])
-            toks = slice(P * r, P * r + P)
-            for j in range(4):
-                rows = slice(P * j, P * j + P)
-                for g in range(G):
-                    nc.tensor.matmul_mx(
-                        out=acc[:, j, :],
-                        lhsT=wc_codes[:, g, rows].bitcast(FP8X4),
-                        lhsT_scale=wc_scales[:, g, rows],
-                        rhs=x_codes[:, b, g, toks].bitcast(FP8X4),
-                        rhs_scale=x_scales[:, b, g, toks],
-                        start=(g == 0),
-                        stop=(g == G - 1),
+        def flips_wb(v, half):
+            heads = range(8 * half, 8 * half + 8)
+            flips(
+                [
+                    [
+                        words(wb_sb[(v, half)][:, h % 8, :], P * u)
+                        for h in (h0, h0 + 1)
+                        for u in range(2)
+                    ]
+                    for h0 in heads
+                    if h0 % 2 == 0
+                ],
+                [
+                    (
+                        wb_codes[:, v, 512 * hq : 512 * hq + 512],
+                        wb_scales[:, v, 512 * hq : 512 * hq + 512],
                     )
+                    for hq in (2 * half, 2 * half + 1)
+                ],
+                WB_OUT,
+            )
 
-        def stage1_out(b, r, engine):
-            kvg = stage.tile([P, P, 4], BF16, name="kvg%d%d" % (b, r), tag="kvg", bufs=3, align_bytes=64)
-            live["kvg%d%d" % (b, r)] = kvg
-            evac(engine, kvg[:], live["M1%d%d" % (b, r)][:].rearrange("q j t -> q t j"))
-
-        def stage1_quantise(b, r):
+        def stage1_quantise(b, r, grouped):
             toks = slice(P * r, P * r + P)
             nc.vector.quantize_mx(
                 out=kv_codes[:, b, toks].bitcast(FP8X4),
                 scales=kv_scales[:, b, toks],
-                in_=live["kvg%d%d" % (b, r)][:].rearrange("q t j -> q (t j)"),
+                in_=grouped[:].rearrange("q t j -> q (t j)"),
             )
 
-        def product(b, r, v, hq, ps):
-            t = bank("M2%d%d%d%d" % (b, r, v, hq), ps, [P, 512])
+        def stage1(b):
+            for r in range(2):
+                acc = next_bank([P, 4, P])
+                toks = slice(P * r, P * r + P)
+                for j in range(4):
+                    rows = slice(P * j, P * j + P)
+                    for g in range(G):
+                        nc.tensor.matmul_mx(
+                            out=acc[:, j, :],
+                            lhsT=wc_codes[:, g, rows].bitcast(FP8X4),
+                            lhsT_scale=wc_scales[:, g, rows],
+                            rhs=x_codes[:, b, g, toks].bitcast(FP8X4),
+                            rhs_scale=x_scales[:, b, g, toks],
+                            start=(g == 0),
+                            stop=(g == G - 1),
+                        )
+                grouped = stage.tile(
+                    [P, P, 4], BF16, name="kv_grouped%d%d" % (b, r), tag="kv_grouped", bufs=3, align_bytes=64
+                )
+                empty(STAGE1_OUT[r], grouped[:], acc[:].rearrange("q j t -> q t j"))
+                later(LAG_STAGE1_QUANTISE, stage1_quantise, b, r, grouped)
+                job_done()
+
+        def product(b, r, v, hq):
+            bank = next_bank([P, 512])
             toks = slice(P * r, P * r + P)
             cols = slice(512 * hq, 512 * hq + 512)
             nc.tensor.matmul_mx(
-                out=t[:],
+                out=bank[:],
                 lhsT=kv_codes[:, b, toks].bitcast(FP8X4),
                 lhsT_scale=kv_scales[:, b, toks],
                 rhs=wb_codes[:, v, cols].bitcast(FP8X4),
@@ -550,63 +241,30 @@ def tile_ssa_pb_kernel(tc, x, wkv_c, wkv_b, out_0, out_1):
                 start=True,
                 stop=True,
             )
+            return bank
 
-        def product_out(b, r, v, hq, engine):
-            t = live["M2%d%d%d%d" % (b, r, v, hq)]
-            dst = slab("%s%d%d" % ("av"[v], b, r), [P, H * P], F32)
-            cols = slice(512 * hq, 512 * hq + 512)
-            if v == 0:
-                nc.scalar.activation(out=dst[:, cols], in_=t[:], func=ACT.Silu)
-            else:
-                evac(engine, dst[:, cols], t[:])
+        def store(view, tile_, cols):
+            nc.sync.dma_start(out=view[:, cols], in_=tile_[:, cols])
 
-        def part_max(b, r, h):
-            if "pm%d" % b not in live:
-                live["pm%d" % b] = small.tile([P, 4], F32, name="pm%d" % b, tag="pm")
-            i = 2 * r + h
-            nc.vector.tensor_reduce(
-                out=live["pm%d" % b][:, i : i + 1],
-                in_=live["a%d%d" % (b, r)][:, 1024 * h : 1024 * h + 1024],
-                axis=AX.X,
-                op=ALU.max,
-            )
+        def values(b):
+            for r in range(2):
+                vt = slabs.tile([P, H * P], F32, name="v%d%d" % (b, r), tag="slab")
+                for hq in range(4):
+                    bank = product(b, r, 1, hq)
+                    empty(VALUES_OUT[4 * r + hq], vt[:, 512 * hq : 512 * hq + 512], bank[:])
+                    if hq % 2 == 1:
+                        later(LAG_STORE, store, v_view[b, r], vt, slice(512 * (hq - 1), 512 * (hq + 1)))
+                    job_done()
 
-        def spread_max(b):
-            tokmax = small.tile([P, 1], F32, name="tokmax%d" % b, tag="tokmax")
-            nc.vector.tensor_reduce(out=tokmax[:], in_=live["pm%d" % b][:], axis=AX.X, op=ALU.max)
-            spread = small.tile([P, P], F32, name="spread%d" % b, tag="spread")
+        def part_max(part, i, a, cols):
+            nc.vector.tensor_reduce(out=part[:, i : i + 1], in_=a[:, cols], axis=AX.X, op=ALU.max)
+
+        def spread_max(part, spread):
+            tokmax = small.tile([P, 1], F32, name="tokmax", tag="tokmax")
+            nc.vector.tensor_reduce(out=tokmax[:], in_=part[:], axis=AX.X, op=ALU.max)
             nc.vector.tensor_copy(out=spread[:], in_=tokmax[:].to_broadcast([P, P]))
-            live["spread%d" % b] = spread
 
-        def flip_max(b, ps):
-            t = bank("ET%d" % b, ps, [P, 4, P])
-            nc.tensor.transpose(t[:, 0, :], live["spread%d" % b][:], ident[:])
-
-        def factors(b):
-            m = small.tile([P, H], F32, name="m%d" % b, tag="m")
-            nc.vector.tensor_reduce(
-                out=m[:],
-                in_=live["ET%d" % b][:, 0, :].rearrange("q (g s) -> q g s", s=8),
-                axis=AX.X,
-                op=ALU.max,
-            )
-            z = small.tile([P, H], F32, name="z%d" % b, tag="z")
-            nc.vector.tensor_scalar(
-                out=z[:], in0=m[:], scalar1=0.0, scalar2=1e-6, op0=ALU.is_equal, op1=ALU.mult
-            )
-            nc.vector.tensor_tensor(out=z[:], in0=z[:], in1=m[:], op=ALU.add)
-            rc = small.tile([P, H], F32, name="rc%d" % b, tag="rc")
-            nc.vector.reciprocal(out=rc[:], in_=z[:])
-            eta = small.tile([P, H], F32, name="eta%d" % b, tag="eta")
-            nc.vector.tensor_scalar(
-                out=eta[:], in0=rc[:], scalar1=10.0, scalar2=1.0, op0=ALU.mult, op1=ALU.min
-            )
-            live["eta%d" % b] = eta
-
-        def scale_heads(b, r, k, engine):
-            n = H // len(MUL[b])
-            h0 = n * k
-            a, eta = live["a%d%d" % (b, r)], live["eta%d" % b]
+        def scale_heads(engine, a, eta, h0, n):
             a3 = a[:, P * h0 : P * (h0 + n)].rearrange("p (h d) -> p h d", h=n)
             e3 = eta[:, h0 : h0 + n].unsqueeze(2).to_broadcast([P, n, P])
             if engine == "g":
@@ -622,47 +280,72 @@ def tile_ssa_pb_kernel(tc, x, wkv_c, wkv_b, out_0, out_1):
                         scale=eta[:, h : h + 1],
                     )
 
-        def store_keys(b, r, k, pieces):
-            n = pieces * H // len(MUL[b])
-            cols = slice(P * n * k, P * n * (k + 1))
-            nc.sync.dma_start(out=k_view[b, r, :, cols], in_=live["a%d%d" % (b, r)][:, cols])
+        def clamp(b, tiles, spread):
+            bank = next_bank([P, 4, P])
+            nc.tensor.transpose(bank[:, 0, :], spread[:], ident[:])
+            m = small.tile([P, H], F32, name="m", tag="m")
+            nc.vector.tensor_reduce(
+                out=m[:], in_=bank[:, 0, :].rearrange("q (g s) -> q g s", s=8), axis=AX.X, op=ALU.max
+            )
+            z = small.tile([P, H], F32, name="z", tag="z")
+            nc.vector.tensor_scalar(
+                out=z[:], in0=m[:], scalar1=0.0, scalar2=1e-6, op0=ALU.is_equal, op1=ALU.mult
+            )
+            nc.vector.tensor_tensor(out=z[:], in0=z[:], in1=m[:], op=ALU.add)
+            rc = small.tile([P, H], F32, name="rc", tag="rc")
+            nc.vector.reciprocal(out=rc[:], in_=z[:])
+            eta = small.tile([P, H], F32, name="eta", tag="eta")
+            nc.vector.tensor_scalar(
+                out=eta[:], in0=rc[:], scalar1=10.0, scalar2=1.0, op0=ALU.mult, op1=ALU.min
+            )
+            last = b == B - 1
+            engines = CLAMP_LAST if last else CLAMP
+            for r in range(2):
+                for q in range(4):
+                    scale_heads(engines[q], tiles[r], eta, 4 * q, 4)
+            for j in range(4):
+                lag = 1 + j if last else LAG_KEY_STORE + STEP_KEY_STORE * j
+                later(lag, store, k_view[b, j // 2], tiles[j // 2], slice(1024 * (j % 2), 1024 * (j % 2) + 1024))
 
-        def store_values(b, r, h):
-            cols = slice(1024 * h, 1024 * h + 1024)
-            nc.sync.dma_start(out=v_view[b, r, :, cols], in_=live["v%d%d" % (b, r)][:, cols])
+        def keys(b):
+            part = small.tile([P, 4], F32, name="part", tag="part")
+            spread = small.tile([P, P], F32, name="spread", tag="spread")
+            tiles = [slabs.tile([P, H * P], F32, name="a%d%d" % (b, r), tag="slab") for r in range(2)]
+            for r in range(2):
+                for hq in range(4):
+                    bank = product(b, r, 0, hq)
+                    nc.scalar.activation(
+                        out=tiles[r][:, 512 * hq : 512 * hq + 512], in_=bank[:], func=ACT.Silu
+                    )
+                    if hq % 2 == 1:
+                        later(
+                            LAG_MAX, part_max, part, 2 * r + hq // 2, tiles[r], slice(512 * (hq - 1), 512 * (hq + 1))
+                        )
+                    if r == 1 and hq == 3:
+                        later(LAG_MAX, spread_max, part, spread)
+                        later(LAG_FACTORS, clamp, b, tiles, spread)
+                    job_done()
 
-        for name, engine, ps, grp in ORDER:
-            d = [int(c) for c in name if c in "0123456789"]
-            if name[0] == "L":
-                load(name[1:])
-            elif name[0] == "T":
-                flip(name[1:], ps, grp)
-            elif name[0] == "e":
-                flip_out(name[1:], engine)
-            elif name[:3] == "qkv":
-                stage1_quantise(d[0], d[1])
-            elif name[0] == "q":
-                quantise(name[1:])
-            elif name[:2] == "M1":
-                stage1(d[1], d[2], ps)
-            elif name[:3] == "kve":
-                stage1_out(d[0], d[1], engine)
-            elif name[:2] == "M2":
-                product(d[1], d[2], d[3], d[4], ps)
-            elif name[0] == "o":
-                product_out(d[0], d[1], d[2], d[3], engine)
-            elif name[:2] == "mx":
-                part_max(d[0], d[1], d[2])
-            elif name[:2] == "Sv":
-                store_values(d[0], d[1], d[2])
-            elif name[:2] == "E1":
-                spread_max(d[1])
-            elif name[:2] == "ET":
-                flip_max(d[0], ps)
-            elif name[:2] == "E2":
-                factors(d[1])
-            elif name[:2] == "mu":
-                scale_heads(d[0], d[1], d[2], engine)
-            else:
-                assert name[:2] == "Sk"
-                store_keys(d[0], d[1], d[2], 2 if name[-1] == "p" else 1)
+        flips_x(0, X0_OUT)
+        flips_wc()
+        flips_wb(1, 0)
+        flips_x(1, X_OUT)
+        stage1(0)
+        flips_wb(1, 1)
+        flips_wb(0, 0)
+        values(0)
+        flips_wb(0, 1)
+        flips_x(2, X_OUT)
+        keys(0)
+        stage1(1)
+        stage1(2)
+        values(1)
+        flips_x(3, X_OUT)
+        keys(1)
+        stage1(3)
+        values(2)
+        keys(2)
+        values(3)
+        keys(3)
+        while waiting["list"]:
+            job_done()

@@ -14,35 +14,37 @@ AX = mybir.AxisListType
 
 P = 128
 B, S, D, H, KVL = 4, 256, 2048, 16, 512
-G = D // 512
+PASSES = D // 512
+KEYS, VALUES = 0, 1
 FLOPS = 2 * B * S * D * KVL + 2 * B * S * KVL * H * 256
 
 BANKS = 8
 STAGES = 5
-SLABS = 18
+SLOTS = 18
 
-X0_OUT = "svsv"
+X0_OUT = "sssv"
+X_OUT = "svss"
 WC_OUT = "sssvsssv"
 WB_OUT = "svsv"
-X_OUT = "sssv"
-VALUES_OUT = "svssvssv"
 STAGE1_OUT = "ss"
+VALUES_OUT = "svssvssv"
 CLAMP = "gggv"
 CLAMP_LAST = "vgvs"
-LAG_QUANTISE = 3
-LAG_STAGE1_QUANTISE = 2
+
+LAG_QUANTISE = 2
+LAG_STAGE1_QUANTISE = 1
 LAG_MAX = 1
-LAG_STORE = 1
+LAG_STORE = 2
 LAG_FACTORS = 9
 LAG_KEY_STORE = 6
-STEP_KEY_STORE = 7
+STEP_KEY_STORE = 5
 
 
 def tile_ssa_pb_kernel(tc, x, wkv_c, wkv_b, out_0, out_1):
     nc = tc.nc
     with ExitStack() as ctx:
         const = ctx.enter_context(tc.tile_pool(name="const", bufs=1))
-        slabs = ctx.enter_context(tc.tile_pool(name="slabs", bufs=SLABS))
+        slots = ctx.enter_context(tc.tile_pool(name="slots", bufs=SLOTS))
         stage = ctx.enter_context(tc.tile_pool(name="stage", bufs=1))
         keep = ctx.enter_context(tc.tile_pool(name="keep", bufs=1))
         small = ctx.enter_context(tc.tile_pool(name="small", bufs=2))
@@ -58,26 +60,26 @@ def tile_ssa_pb_kernel(tc, x, wkv_c, wkv_b, out_0, out_1):
         x_sb, wc_sb, wb_sb = {}, {}, {}
 
         def load_x(b):
-            x_sb[b] = slabs.tile([P, 2, D], BF16, name="x_sb%d" % b, tag="slab")
+            x_sb[b] = slots.tile([P, 2, D], BF16, name="x_sb%d" % b, tag="slot")
             nc.sync.dma_start(out=x_sb[b][:], in_=x_view[b])
 
         def load_wc(u):
-            wc_sb[u] = slabs.tile([P, 2, D], BF16, name="wc_sb%d" % u, tag="slab")
+            wc_sb[u] = slots.tile([P, 2, D], BF16, name="wc_sb%d" % u, tag="slot")
             nc.sync.dma_start(out=wc_sb[u][:], in_=wc_view[u])
 
         def load_wb(v, half):
-            t = slabs.tile([P, 8, KVL], BF16, name="wb_sb%d%d" % (v, half), tag="slab")
+            t = slots.tile([P, 8, KVL], BF16, name="wb_sb%d%d" % (v, half), tag="slot")
             nc.sync.dma_start(out=t[:], in_=wb_view[v, :, 8 * half : 8 * half + 8, :])
             wb_sb[(v, half)] = t
 
         load_x(0)
         load_wc(0)
         load_wc(1)
-        load_wb(1, 0)
+        load_wb(VALUES, 0)
         load_x(1)
-        load_wb(1, 1)
-        load_wb(0, 0)
-        load_wb(0, 1)
+        load_wb(VALUES, 1)
+        load_wb(KEYS, 0)
+        load_wb(KEYS, 1)
         load_x(2)
         load_x(3)
 
@@ -87,25 +89,25 @@ def tile_ssa_pb_kernel(tc, x, wkv_c, wkv_b, out_0, out_1):
         nc.vector.memset(warm[:], 0.0)
         nc.scalar.activation(out=warm[:, 1:2], in_=warm[:, 0:1], func=ACT.Silu)
 
-        wc_codes = keep.tile([P, G, KVL], U32, name="wc_codes", align_bytes=64)
-        wc_scales = keep.tile([P, G, KVL], U8, name="wc_scales", align_bytes=64)
-        x_codes = keep.tile([P, B, G, S], U32, name="x_codes", align_bytes=64)
-        x_scales = keep.tile([P, B, G, S], U8, name="x_scales", align_bytes=64)
+        wc_codes = keep.tile([P, PASSES, KVL], U32, name="wc_codes", align_bytes=64)
+        wc_scales = keep.tile([P, PASSES, KVL], U8, name="wc_scales", align_bytes=64)
+        x_codes = keep.tile([P, B, PASSES, S], U32, name="x_codes", align_bytes=64)
+        x_scales = keep.tile([P, B, PASSES, S], U8, name="x_scales", align_bytes=64)
         wb_codes = keep.tile([P, 2, H * P], U32, name="wb_codes", align_bytes=64)
         wb_scales = keep.tile([P, 2, H * P], U8, name="wb_scales", align_bytes=64)
         kv_codes = keep.tile([P, B, S], U32, name="kv_codes", align_bytes=64)
         kv_scales = keep.tile([P, B, S], U8, name="kv_scales", align_bytes=64)
 
         count = {"job": 0, "bank": 0, "stage": 0}
-        waiting = {"list": []}
+        waiting = {"steps": []}
 
-        def later(lag, fn, *args):
-            waiting["list"].append((count["job"] + lag, fn, args))
+        def later(lag, step, *args):
+            waiting["steps"].append((count["job"] + lag, step, args))
 
         def job_done():
             count["job"] += 1
-            due = [w for w in waiting["list"] if w[0] <= count["job"]]
-            waiting["list"] = [w for w in waiting["list"] if w[0] > count["job"]]
+            due = [w for w in waiting["steps"] if w[0] <= count["job"]]
+            waiting["steps"] = [w for w in waiting["steps"] if w[0] > count["job"]]
             for w in due:
                 w[1](*w[2])
 
@@ -124,11 +126,11 @@ def tile_ssa_pb_kernel(tc, x, wkv_c, wkv_b, out_0, out_1):
             return ap.bitcast(F32)[:, first : first + P]
 
         def quantise(grouped, codes, scales):
-            nc.vector.quantize_mx(out=codes.bitcast(FP8X4), scales=scales, in_=grouped[:])
+            nc.vector.quantize_mx(out=codes.bitcast(FP8X4), scales=scales, in_=grouped)
 
-        def flips(banks, targets, engines):
+        def transposes(jobs, targets, engines):
             grouped = None
-            for i in range(len(banks)):
+            for i in range(len(jobs)):
                 if i % 2 == 0:
                     n = count["stage"]
                     count["stage"] += 1
@@ -137,72 +139,55 @@ def tile_ssa_pb_kernel(tc, x, wkv_c, wkv_b, out_0, out_1):
                     )
                 bank = next_bank([P, 4, P])
                 for j in range(4):
-                    nc.tensor.transpose(bank[:, j, :], banks[i][j], ident[:])
-                half = 2 * (i % 2)
+                    nc.tensor.transpose(bank[:, j, :], jobs[i][j], ident[:])
+                first = 2 * (i % 2)
                 empty(
-                    engines[i % len(engines)],
-                    grouped[:].bitcast(F32).rearrange("q (a c u) -> q a c u", a=4, u=2)[:, half : half + 2],
+                    engines[i],
+                    grouped[:].bitcast(F32).rearrange("q (a c u) -> q a c u", a=4, u=2)[:, first : first + 2],
                     bank[:].rearrange("q (a u) c -> q a c u", u=2),
                 )
                 if i % 2 == 1:
-                    later(LAG_QUANTISE, quantise, grouped, targets[i // 2][0], targets[i // 2][1])
+                    later(LAG_QUANTISE, quantise, grouped[:], targets[i // 2][0], targets[i // 2][1])
                 job_done()
 
-        def flips_x(b, engines):
-            flips(
+        def transpose_x(b, engines):
+            transposes(
                 [
                     [words(x_sb[b][:, r, :], 256 * g + P * u) for r in range(2) for u in range(2)]
-                    for g in range(G)
+                    for g in range(PASSES)
                 ],
                 [
                     (
-                        x_codes[:, b, 2 * gp : 2 * gp + 2, :].rearrange("q g s -> q (g s)"),
-                        x_scales[:, b, 2 * gp : 2 * gp + 2, :].rearrange("q g s -> q (g s)"),
+                        x_codes[:, b, g : g + 2, :].rearrange("q g s -> q (g s)"),
+                        x_scales[:, b, g : g + 2, :].rearrange("q g s -> q (g s)"),
                     )
-                    for gp in range(2)
+                    for g in (0, 2)
                 ],
                 engines,
             )
 
-        def flips_wc():
-            flips(
+        def transpose_wc():
+            transposes(
                 [
                     [words(wc_sb[u][:, e, :], 256 * g + P * u2) for e in range(2) for u2 in range(2)]
-                    for g in range(G)
+                    for g in range(PASSES)
                     for u in range(2)
                 ],
-                [(wc_codes[:, g, :], wc_scales[:, g, :]) for g in range(G)],
+                [(wc_codes[:, g, :], wc_scales[:, g, :]) for g in range(PASSES)],
                 WC_OUT,
             )
 
-        def flips_wb(v, half):
-            heads = range(8 * half, 8 * half + 8)
-            flips(
+        def transpose_wb(v, half):
+            transposes(
                 [
-                    [
-                        words(wb_sb[(v, half)][:, h % 8, :], P * u)
-                        for h in (h0, h0 + 1)
-                        for u in range(2)
-                    ]
-                    for h0 in heads
-                    if h0 % 2 == 0
+                    [words(wb_sb[(v, half)][:, h, :], P * u) for h in (h0, h0 + 1) for u in range(2)]
+                    for h0 in (0, 2, 4, 6)
                 ],
                 [
-                    (
-                        wb_codes[:, v, 512 * hq : 512 * hq + 512],
-                        wb_scales[:, v, 512 * hq : 512 * hq + 512],
-                    )
-                    for hq in (2 * half, 2 * half + 1)
+                    (wb_codes[:, v, 512 * n : 512 * n + 512], wb_scales[:, v, 512 * n : 512 * n + 512])
+                    for n in (2 * half, 2 * half + 1)
                 ],
                 WB_OUT,
-            )
-
-        def stage1_quantise(b, r, grouped):
-            toks = slice(P * r, P * r + P)
-            nc.vector.quantize_mx(
-                out=kv_codes[:, b, toks].bitcast(FP8X4),
-                scales=kv_scales[:, b, toks],
-                in_=grouped[:].rearrange("q t j -> q (t j)"),
             )
 
         def stage1(b):
@@ -211,7 +196,7 @@ def tile_ssa_pb_kernel(tc, x, wkv_c, wkv_b, out_0, out_1):
                 toks = slice(P * r, P * r + P)
                 for j in range(4):
                     rows = slice(P * j, P * j + P)
-                    for g in range(G):
+                    for g in range(PASSES):
                         nc.tensor.matmul_mx(
                             out=acc[:, j, :],
                             lhsT=wc_codes[:, g, rows].bitcast(FP8X4),
@@ -219,19 +204,25 @@ def tile_ssa_pb_kernel(tc, x, wkv_c, wkv_b, out_0, out_1):
                             rhs=x_codes[:, b, g, toks].bitcast(FP8X4),
                             rhs_scale=x_scales[:, b, g, toks],
                             start=(g == 0),
-                            stop=(g == G - 1),
+                            stop=(g == PASSES - 1),
                         )
                 grouped = stage.tile(
                     [P, P, 4], BF16, name="kv_grouped%d%d" % (b, r), tag="kv_grouped", bufs=3, align_bytes=64
                 )
                 empty(STAGE1_OUT[r], grouped[:], acc[:].rearrange("q j t -> q t j"))
-                later(LAG_STAGE1_QUANTISE, stage1_quantise, b, r, grouped)
+                later(
+                    LAG_STAGE1_QUANTISE,
+                    quantise,
+                    grouped[:].rearrange("q t j -> q (t j)"),
+                    kv_codes[:, b, toks],
+                    kv_scales[:, b, toks],
+                )
                 job_done()
 
-        def product(b, r, v, hq):
+        def product(b, r, v, n):
             bank = next_bank([P, 512])
             toks = slice(P * r, P * r + P)
-            cols = slice(512 * hq, 512 * hq + 512)
+            cols = slice(512 * n, 512 * n + 512)
             nc.tensor.matmul_mx(
                 out=bank[:],
                 lhsT=kv_codes[:, b, toks].bitcast(FP8X4),
@@ -248,104 +239,98 @@ def tile_ssa_pb_kernel(tc, x, wkv_c, wkv_b, out_0, out_1):
 
         def values(b):
             for r in range(2):
-                vt = slabs.tile([P, H * P], F32, name="v%d%d" % (b, r), tag="slab")
-                for hq in range(4):
-                    bank = product(b, r, 1, hq)
-                    empty(VALUES_OUT[4 * r + hq], vt[:, 512 * hq : 512 * hq + 512], bank[:])
-                    if hq % 2 == 1:
-                        later(LAG_STORE, store, v_view[b, r], vt, slice(512 * (hq - 1), 512 * (hq + 1)))
+                v_sb = slots.tile([P, H * P], F32, name="v_sb%d%d" % (b, r), tag="slot")
+                for n in range(4):
+                    bank = product(b, r, VALUES, n)
+                    empty(VALUES_OUT[4 * r + n], v_sb[:, 512 * n : 512 * n + 512], bank[:])
+                    if n % 2 == 1:
+                        later(LAG_STORE, store, v_view[b, r], v_sb, slice(512 * (n - 1), 512 * (n + 1)))
                     job_done()
 
-        def part_max(part, i, a, cols):
-            nc.vector.tensor_reduce(out=part[:, i : i + 1], in_=a[:, cols], axis=AX.X, op=ALU.max)
+        def part_max(part, i, a_sb, cols):
+            nc.vector.tensor_reduce(out=part[:, i : i + 1], in_=a_sb[:, cols], axis=AX.X, op=ALU.max)
 
         def spread_max(part, spread):
-            tokmax = small.tile([P, 1], F32, name="tokmax", tag="tokmax")
-            nc.vector.tensor_reduce(out=tokmax[:], in_=part[:], axis=AX.X, op=ALU.max)
-            nc.vector.tensor_copy(out=spread[:], in_=tokmax[:].to_broadcast([P, P]))
+            both = small.tile([P, 1], F32, name="both", tag="both")
+            nc.vector.tensor_reduce(out=both[:], in_=part[:], axis=AX.X, op=ALU.max)
+            nc.vector.tensor_copy(out=spread[:], in_=both[:].to_broadcast([P, P]))
 
-        def scale_heads(engine, a, eta, h0, n):
-            a3 = a[:, P * h0 : P * (h0 + n)].rearrange("p (h d) -> p h d", h=n)
-            e3 = eta[:, h0 : h0 + n].unsqueeze(2).to_broadcast([P, n, P])
+        def scale_heads(engine, a_sb, eta, h0):
+            a3 = a_sb[:, P * h0 : P * (h0 + 4)].rearrange("p (h d) -> p h d", h=4)
+            e3 = eta[:, h0 : h0 + 4].unsqueeze(2).to_broadcast([P, 4, P])
             if engine == "g":
                 nc.gpsimd.tensor_tensor(out=a3, in0=a3, in1=e3, op=ALU.mult)
             elif engine == "v":
                 nc.vector.tensor_tensor(out=a3, in0=a3, in1=e3, op=ALU.mult)
             else:
-                for h in range(h0, h0 + n):
+                for h in range(h0, h0 + 4):
                     nc.scalar.activation(
-                        out=a[:, P * h : P * h + P],
-                        in_=a[:, P * h : P * h + P],
+                        out=a_sb[:, P * h : P * h + P],
+                        in_=a_sb[:, P * h : P * h + P],
                         func=ACT.Copy,
                         scale=eta[:, h : h + 1],
                     )
 
-        def clamp(b, tiles, spread):
+        def clamp(b, a_sb, spread):
             bank = next_bank([P, 4, P])
             nc.tensor.transpose(bank[:, 0, :], spread[:], ident[:])
             m = small.tile([P, H], F32, name="m", tag="m")
             nc.vector.tensor_reduce(
                 out=m[:], in_=bank[:, 0, :].rearrange("q (g s) -> q g s", s=8), axis=AX.X, op=ALU.max
             )
-            z = small.tile([P, H], F32, name="z", tag="z")
+            safe = small.tile([P, H], F32, name="safe", tag="safe")
             nc.vector.tensor_scalar(
-                out=z[:], in0=m[:], scalar1=0.0, scalar2=1e-6, op0=ALU.is_equal, op1=ALU.mult
+                out=safe[:], in0=m[:], scalar1=0.0, scalar2=1e-6, op0=ALU.is_equal, op1=ALU.mult
             )
-            nc.vector.tensor_tensor(out=z[:], in0=z[:], in1=m[:], op=ALU.add)
-            rc = small.tile([P, H], F32, name="rc", tag="rc")
-            nc.vector.reciprocal(out=rc[:], in_=z[:])
+            nc.vector.tensor_tensor(out=safe[:], in0=safe[:], in1=m[:], op=ALU.add)
+            inverse = small.tile([P, H], F32, name="inverse", tag="inverse")
+            nc.vector.reciprocal(out=inverse[:], in_=safe[:])
             eta = small.tile([P, H], F32, name="eta", tag="eta")
             nc.vector.tensor_scalar(
-                out=eta[:], in0=rc[:], scalar1=10.0, scalar2=1.0, op0=ALU.mult, op1=ALU.min
+                out=eta[:], in0=inverse[:], scalar1=10.0, scalar2=1.0, op0=ALU.mult, op1=ALU.min
             )
             last = b == B - 1
-            engines = CLAMP_LAST if last else CLAMP
             for r in range(2):
-                for q in range(4):
-                    scale_heads(engines[q], tiles[r], eta, 4 * q, 4)
-            for j in range(4):
-                lag = 1 + j if last else LAG_KEY_STORE + STEP_KEY_STORE * j
-                later(lag, store, k_view[b, j // 2], tiles[j // 2], slice(1024 * (j % 2), 1024 * (j % 2) + 1024))
+                for n in range(4):
+                    scale_heads((CLAMP_LAST if last else CLAMP)[n], a_sb[r], eta, 4 * n)
+            for i in range(4):
+                lag = 1 + i if last else LAG_KEY_STORE + STEP_KEY_STORE * i
+                later(lag, store, k_view[b, i // 2], a_sb[i // 2], slice(1024 * (i % 2), 1024 * (i % 2) + 1024))
 
         def keys(b):
             part = small.tile([P, 4], F32, name="part", tag="part")
             spread = small.tile([P, P], F32, name="spread", tag="spread")
-            tiles = [slabs.tile([P, H * P], F32, name="a%d%d" % (b, r), tag="slab") for r in range(2)]
+            a_sb = [slots.tile([P, H * P], F32, name="a_sb%d%d" % (b, r), tag="slot") for r in range(2)]
             for r in range(2):
-                for hq in range(4):
-                    bank = product(b, r, 0, hq)
-                    nc.scalar.activation(
-                        out=tiles[r][:, 512 * hq : 512 * hq + 512], in_=bank[:], func=ACT.Silu
-                    )
-                    if hq % 2 == 1:
-                        later(
-                            LAG_MAX, part_max, part, 2 * r + hq // 2, tiles[r], slice(512 * (hq - 1), 512 * (hq + 1))
-                        )
-                    if r == 1 and hq == 3:
+                for n in range(4):
+                    bank = product(b, r, KEYS, n)
+                    nc.scalar.activation(out=a_sb[r][:, 512 * n : 512 * n + 512], in_=bank[:], func=ACT.Silu)
+                    if n % 2 == 1:
+                        later(LAG_MAX, part_max, part, 2 * r + n // 2, a_sb[r], slice(512 * (n - 1), 512 * (n + 1)))
+                    if r == 1 and n == 3:
                         later(LAG_MAX, spread_max, part, spread)
-                        later(LAG_FACTORS, clamp, b, tiles, spread)
+                        later(LAG_FACTORS, clamp, b, a_sb, spread)
                     job_done()
 
-        flips_x(0, X0_OUT)
-        flips_wc()
-        flips_wb(1, 0)
-        flips_x(1, X_OUT)
+        transpose_x(0, X0_OUT)
+        transpose_wc()
+        transpose_wb(VALUES, 0)
+        transpose_x(1, X_OUT)
         stage1(0)
-        flips_wb(1, 1)
-        flips_wb(0, 0)
+        transpose_wb(VALUES, 1)
+        transpose_wb(KEYS, 0)
         values(0)
-        flips_wb(0, 1)
-        flips_x(2, X_OUT)
+        transpose_wb(KEYS, 1)
+        transpose_x(2, X_OUT)
         keys(0)
         stage1(1)
+        transpose_x(3, X_OUT)
         stage1(2)
         values(1)
-        flips_x(3, X_OUT)
         keys(1)
         stage1(3)
-        values(2)
-        keys(2)
-        values(3)
-        keys(3)
-        while waiting["list"]:
+        for b in (2, 3):
+            values(b)
+            keys(b)
+        while waiting["steps"]:
             job_done()

from contextlib import ExitStack

import concourse.mybir as mybir
from concourse.masks import make_identity

F32 = mybir.dt.float32
BF16 = mybir.dt.bfloat16
U32 = mybir.dt.uint32
U8 = mybir.dt.uint8
FP8X4 = mybir.dt.float8_e4m3fn_x4
ACT = mybir.ActivationFunctionType
ALU = mybir.AluOpType
AX = mybir.AxisListType

P = 128
B, S, D, H, KVL = 4, 256, 2048, 16, 512
PASSES = D // 512
KEYS, VALUES = 0, 1
FLOPS = 2 * B * S * D * KVL + 2 * B * S * KVL * H * 256

BANKS = 8
STAGES = 5
SLOTS = 18

X0_OUT = "sssv"
X_OUT = "svss"
WC_OUT = "sssvsssv"
WB_OUT = "svsv"
STAGE1_OUT = "ss"
VALUES_OUT = "svssvssv"
CLAMP = "gggv"
CLAMP_LAST = "vgvs"

LAG_QUANTISE = 2
LAG_STAGE1_QUANTISE = 1
LAG_MAX = 1
LAG_STORE = 2
LAG_FACTORS = 9
LAG_KEY_STORE = 6
STEP_KEY_STORE = 5


def tile_ssa_pb_kernel(tc, x, wkv_c, wkv_b, out_0, out_1):
    nc = tc.nc
    with ExitStack() as ctx:
        const = ctx.enter_context(tc.tile_pool(name="const", bufs=1))
        slots = ctx.enter_context(tc.tile_pool(name="slots", bufs=SLOTS))
        stage = ctx.enter_context(tc.tile_pool(name="stage", bufs=1))
        keep = ctx.enter_context(tc.tile_pool(name="keep", bufs=1))
        small = ctx.enter_context(tc.tile_pool(name="small", bufs=2))
        psum = ctx.enter_context(tc.psum_pool(name="psum", bufs=1))
        ctx.enter_context(tc.manual_schedule())

        x_view = x.rearrange("b (p r) d -> b p r d", r=2)
        wc_view = wkv_c.rearrange("(u p e) d -> u p e d", u=2, e=2)
        wb_view = wkv_b.rearrange("(h v c) k -> v c h k", v=2, c=P)
        k_view = out_0.rearrange("b (p r) h d -> b r p (h d)", r=2)
        v_view = out_1.rearrange("b (p r) h d -> b r p (h d)", r=2)

        x_sb, wc_sb, wb_sb = {}, {}, {}

        def load_x(b):
            x_sb[b] = slots.tile([P, 2, D], BF16, name="x_sb%d" % b, tag="slot")
            nc.sync.dma_start(out=x_sb[b][:], in_=x_view[b])

        def load_wc(u):
            wc_sb[u] = slots.tile([P, 2, D], BF16, name="wc_sb%d" % u, tag="slot")
            nc.sync.dma_start(out=wc_sb[u][:], in_=wc_view[u])

        def load_wb(v, half):
            t = slots.tile([P, 8, KVL], BF16, name="wb_sb%d%d" % (v, half), tag="slot")
            nc.sync.dma_start(out=t[:], in_=wb_view[v, :, 8 * half : 8 * half + 8, :])
            wb_sb[(v, half)] = t

        load_x(0)
        load_wc(0)
        load_wc(1)
        load_wb(VALUES, 0)
        load_x(1)
        load_wb(VALUES, 1)
        load_wb(KEYS, 0)
        load_wb(KEYS, 1)
        load_x(2)
        load_x(3)

        ident = const.tile([P, P], F32, name="ident")
        make_identity(nc, ident[:])
        warm = const.tile([P, 2], F32, name="warm")
        nc.vector.memset(warm[:], 0.0)
        nc.scalar.activation(out=warm[:, 1:2], in_=warm[:, 0:1], func=ACT.Silu)

        wc_codes = keep.tile([P, PASSES, KVL], U32, name="wc_codes", align_bytes=64)
        wc_scales = keep.tile([P, PASSES, KVL], U8, name="wc_scales", align_bytes=64)
        x_codes = keep.tile([P, B, PASSES, S], U32, name="x_codes", align_bytes=64)
        x_scales = keep.tile([P, B, PASSES, S], U8, name="x_scales", align_bytes=64)
        wb_codes = keep.tile([P, 2, H * P], U32, name="wb_codes", align_bytes=64)
        wb_scales = keep.tile([P, 2, H * P], U8, name="wb_scales", align_bytes=64)
        kv_codes = keep.tile([P, B, S], U32, name="kv_codes", align_bytes=64)
        kv_scales = keep.tile([P, B, S], U8, name="kv_scales", align_bytes=64)

        count = {"job": 0, "bank": 0, "stage": 0}
        waiting = {"steps": []}

        def later(lag, step, *args):
            waiting["steps"].append((count["job"] + lag, step, args))

        def job_done():
            count["job"] += 1
            due = [w for w in waiting["steps"] if w[0] <= count["job"]]
            waiting["steps"] = [w for w in waiting["steps"] if w[0] > count["job"]]
            for w in due:
                w[1](*w[2])

        def next_bank(shape):
            n = count["bank"]
            count["bank"] += 1
            return psum.tile(shape, F32, name="bank%d" % n, tag="bank%d" % (n % BANKS))

        def empty(engine, out, in_):
            if engine == "v":
                nc.vector.tensor_copy(out=out, in_=in_)
            else:
                nc.scalar.copy(out=out, in_=in_)

        def words(ap, first):
            return ap.bitcast(F32)[:, first : first + P]

        def quantise(grouped, codes, scales):
            nc.vector.quantize_mx(out=codes.bitcast(FP8X4), scales=scales, in_=grouped)

        def transposes(jobs, targets, engines):
            grouped = None
            for i in range(len(jobs)):
                if i % 2 == 0:
                    n = count["stage"]
                    count["stage"] += 1
                    grouped = stage.tile(
                        [P, 2048], BF16, name="grouped%d" % n, tag="stage%d" % (n % STAGES), align_bytes=64
                    )
                bank = next_bank([P, 4, P])
                for j in range(4):
                    nc.tensor.transpose(bank[:, j, :], jobs[i][j], ident[:])
                first = 2 * (i % 2)
                empty(
                    engines[i],
                    grouped[:].bitcast(F32).rearrange("q (a c u) -> q a c u", a=4, u=2)[:, first : first + 2],
                    bank[:].rearrange("q (a u) c -> q a c u", u=2),
                )
                if i % 2 == 1:
                    later(LAG_QUANTISE, quantise, grouped[:], targets[i // 2][0], targets[i // 2][1])
                job_done()

        def transpose_x(b, engines):
            transposes(
                [
                    [words(x_sb[b][:, r, :], 256 * g + P * u) for r in range(2) for u in range(2)]
                    for g in range(PASSES)
                ],
                [
                    (
                        x_codes[:, b, g : g + 2, :].rearrange("q g s -> q (g s)"),
                        x_scales[:, b, g : g + 2, :].rearrange("q g s -> q (g s)"),
                    )
                    for g in (0, 2)
                ],
                engines,
            )

        def transpose_wc():
            transposes(
                [
                    [words(wc_sb[u][:, e, :], 256 * g + P * u2) for e in range(2) for u2 in range(2)]
                    for g in range(PASSES)
                    for u in range(2)
                ],
                [(wc_codes[:, g, :], wc_scales[:, g, :]) for g in range(PASSES)],
                WC_OUT,
            )

        def transpose_wb(v, half):
            transposes(
                [
                    [words(wb_sb[(v, half)][:, h, :], P * u) for h in (h0, h0 + 1) for u in range(2)]
                    for h0 in (0, 2, 4, 6)
                ],
                [
                    (wb_codes[:, v, 512 * n : 512 * n + 512], wb_scales[:, v, 512 * n : 512 * n + 512])
                    for n in (2 * half, 2 * half + 1)
                ],
                WB_OUT,
            )

        def stage1(b):
            for r in range(2):
                acc = next_bank([P, 4, P])
                toks = slice(P * r, P * r + P)
                for j in range(4):
                    rows = slice(P * j, P * j + P)
                    for g in range(PASSES):
                        nc.tensor.matmul_mx(
                            out=acc[:, j, :],
                            lhsT=wc_codes[:, g, rows].bitcast(FP8X4),
                            lhsT_scale=wc_scales[:, g, rows],
                            rhs=x_codes[:, b, g, toks].bitcast(FP8X4),
                            rhs_scale=x_scales[:, b, g, toks],
                            start=(g == 0),
                            stop=(g == PASSES - 1),
                        )
                grouped = stage.tile(
                    [P, P, 4], BF16, name="kv_grouped%d%d" % (b, r), tag="kv_grouped", bufs=3, align_bytes=64
                )
                empty(STAGE1_OUT[r], grouped[:], acc[:].rearrange("q j t -> q t j"))
                later(
                    LAG_STAGE1_QUANTISE,
                    quantise,
                    grouped[:].rearrange("q t j -> q (t j)"),
                    kv_codes[:, b, toks],
                    kv_scales[:, b, toks],
                )
                job_done()

        def product(b, r, v, n):
            bank = next_bank([P, 512])
            toks = slice(P * r, P * r + P)
            cols = slice(512 * n, 512 * n + 512)
            nc.tensor.matmul_mx(
                out=bank[:],
                lhsT=kv_codes[:, b, toks].bitcast(FP8X4),
                lhsT_scale=kv_scales[:, b, toks],
                rhs=wb_codes[:, v, cols].bitcast(FP8X4),
                rhs_scale=wb_scales[:, v, cols],
                start=True,
                stop=True,
            )
            return bank

        def store(view, tile_, cols):
            nc.sync.dma_start(out=view[:, cols], in_=tile_[:, cols])

        def values(b):
            for r in range(2):
                v_sb = slots.tile([P, H * P], F32, name="v_sb%d%d" % (b, r), tag="slot")
                for n in range(4):
                    bank = product(b, r, VALUES, n)
                    empty(VALUES_OUT[4 * r + n], v_sb[:, 512 * n : 512 * n + 512], bank[:])
                    if n % 2 == 1:
                        later(LAG_STORE, store, v_view[b, r], v_sb, slice(512 * (n - 1), 512 * (n + 1)))
                    job_done()

        def part_max(part, i, a_sb, cols):
            nc.vector.tensor_reduce(out=part[:, i : i + 1], in_=a_sb[:, cols], axis=AX.X, op=ALU.max)

        def spread_max(part, spread):
            both = small.tile([P, 1], F32, name="both", tag="both")
            nc.vector.tensor_reduce(out=both[:], in_=part[:], axis=AX.X, op=ALU.max)
            nc.vector.tensor_copy(out=spread[:], in_=both[:].to_broadcast([P, P]))

        def scale_heads(engine, a_sb, eta, h0):
            a3 = a_sb[:, P * h0 : P * (h0 + 4)].rearrange("p (h d) -> p h d", h=4)
            e3 = eta[:, h0 : h0 + 4].unsqueeze(2).to_broadcast([P, 4, P])
            if engine == "g":
                nc.gpsimd.tensor_tensor(out=a3, in0=a3, in1=e3, op=ALU.mult)
            elif engine == "v":
                nc.vector.tensor_tensor(out=a3, in0=a3, in1=e3, op=ALU.mult)
            else:
                for h in range(h0, h0 + 4):
                    nc.scalar.activation(
                        out=a_sb[:, P * h : P * h + P],
                        in_=a_sb[:, P * h : P * h + P],
                        func=ACT.Copy,
                        scale=eta[:, h : h + 1],
                    )

        def clamp(b, a_sb, spread):
            bank = next_bank([P, 4, P])
            nc.tensor.transpose(bank[:, 0, :], spread[:], ident[:])
            m = small.tile([P, H], F32, name="m", tag="m")
            nc.vector.tensor_reduce(
                out=m[:], in_=bank[:, 0, :].rearrange("q (g s) -> q g s", s=8), axis=AX.X, op=ALU.max
            )
            safe = small.tile([P, H], F32, name="safe", tag="safe")
            nc.vector.tensor_scalar(
                out=safe[:], in0=m[:], scalar1=0.0, scalar2=1e-6, op0=ALU.is_equal, op1=ALU.mult
            )
            nc.vector.tensor_tensor(out=safe[:], in0=safe[:], in1=m[:], op=ALU.add)
            inverse = small.tile([P, H], F32, name="inverse", tag="inverse")
            nc.vector.reciprocal(out=inverse[:], in_=safe[:])
            eta = small.tile([P, H], F32, name="eta", tag="eta")
            nc.vector.tensor_scalar(
                out=eta[:], in0=inverse[:], scalar1=10.0, scalar2=1.0, op0=ALU.mult, op1=ALU.min
            )
            last = b == B - 1
            for r in range(2):
                for n in range(4):
                    scale_heads((CLAMP_LAST if last else CLAMP)[n], a_sb[r], eta, 4 * n)
            for i in range(4):
                lag = 1 + i if last else LAG_KEY_STORE + STEP_KEY_STORE * i
                later(lag, store, k_view[b, i // 2], a_sb[i // 2], slice(1024 * (i % 2), 1024 * (i % 2) + 1024))

        def keys(b):
            part = small.tile([P, 4], F32, name="part", tag="part")
            spread = small.tile([P, P], F32, name="spread", tag="spread")
            a_sb = [slots.tile([P, H * P], F32, name="a_sb%d%d" % (b, r), tag="slot") for r in range(2)]
            for r in range(2):
                for n in range(4):
                    bank = product(b, r, KEYS, n)
                    nc.scalar.activation(out=a_sb[r][:, 512 * n : 512 * n + 512], in_=bank[:], func=ACT.Silu)
                    if n % 2 == 1:
                        later(LAG_MAX, part_max, part, 2 * r + n // 2, a_sb[r], slice(512 * (n - 1), 512 * (n + 1)))
                    if r == 1 and n == 3:
                        later(LAG_MAX, spread_max, part, spread)
                        later(LAG_FACTORS, clamp, b, a_sb, spread)
                    job_done()

        transpose_x(0, X0_OUT)
        transpose_wc()
        transpose_wb(VALUES, 0)
        transpose_x(1, X_OUT)
        stage1(0)
        transpose_wb(VALUES, 1)
        transpose_wb(KEYS, 0)
        values(0)
        transpose_wb(KEYS, 1)
        transpose_x(2, X_OUT)
        keys(0)
        stage1(1)
        transpose_x(3, X_OUT)
        stage1(2)
        values(1)
        keys(1)
        stage1(3)
        for b in (2, 3):
            values(b)
            keys(b)
        while waiting["steps"]:
            job_done()
